import numpy as np
import ml_dtypes


def mxq(x, axis, fmt="e4m3"):
    dtype, down = {"e4m3": (ml_dtypes.float8_e4m3fn, 7), "e5m2": (ml_dtypes.float8_e5m2, 14)}[fmt]
    v = np.moveaxis(np.asarray(x, np.float32).astype(ml_dtypes.bfloat16).astype(np.float64), axis, -1)
    blocks = v.reshape(v.shape[:-1] + (-1, 32))
    amax = np.abs(blocks).max(-1, keepdims=True)
    byte = np.maximum(np.where(amax > 0, np.frexp(amax)[1] - 1 + 127, 0) - down, 1)
    scale = np.exp2(byte - 127.0)
    codes = (blocks / scale).astype(np.float32).astype(dtype).astype(np.float64)
    return np.moveaxis((codes * scale).reshape(v.shape), -1, axis)


WIDE = False


def mx_kscale(k):
    if not WIDE:
        return np.ones(k)
    levels = np.array([10, -10, 5, -5, 0])
    if k % 512:
        return np.exp2(np.random.permutation(np.resize(levels, k // 32))).repeat(32)
    a = np.empty((k // 512, 16))
    for p in range(k // 512):
        a[p, :8] = np.random.permutation(np.resize(levels, 8))
        for g in range(8):
            far = levels[np.abs(levels - a[p, g]) >= 10]
            a[p, g + 8] = far[np.random.randint(len(far))]
    return np.exp2(a.ravel()).repeat(32)


BF16 = ml_dtypes.bfloat16


def bf(x):
    return np.asarray(x, np.float32).astype(BF16)


def f64(x):
    return np.asarray(x).astype(np.float64)


B, A, S, F = 512, 16, 256, 512


def draw0():
    s, u = mx_kscale(F), mx_kscale(F)
    t, v = mx_kscale(F), mx_kscale(F)
    return {
        "h1": bf(np.maximum(np.random.standard_normal((B, A, F)) * 1.4, 0.0) * s),
        "W2": bf(np.random.standard_normal((A, F, F)) * 1.4 / np.sqrt(F) / s[:, None] * t),
        "b2": bf(np.random.standard_normal((A, F)) * 0.2 * t),
        "W3": bf(np.random.standard_normal((A, F, S)) / np.sqrt(F) / t[:, None]),
        "b3": bf(np.random.standard_normal((A, S)) * 0.2),
        "g1": bf(np.maximum(np.random.standard_normal((B, F)) * 1.4, 0.0) * u),
        "V2": bf(np.random.standard_normal((F, F)) * 1.4 / np.sqrt(F) / u[:, None] * v),
        "c2": bf(np.random.standard_normal(F) * 0.2 * v),
        "V3": bf(np.random.standard_normal((F, S)) / np.sqrt(F) / v[:, None]),
        "c3": bf(np.random.standard_normal(S) * 0.2),
    }


def core(h1, W2, b2, W3, b3, g1, V2, c2, V3, c3):
    ha = mxq(f64(h1), 2, "e4m3").transpose(1, 0, 2)
    h2 = np.maximum((ha @ mxq(f64(W2), 1, "e4m3")) + f64(b2)[:, None, :], 0.0)
    psi_adv = ((mxq(h2, 2, "e4m3") @ mxq(f64(W3), 1, "e4m3")) + f64(b3)[:, None, :]).transpose(1, 0, 2)
    g2 = np.maximum((mxq(f64(g1), 1, "e4m3") @ mxq(f64(V2), 0, "e4m3")) + f64(c2), 0.0)
    psi_state = (mxq(g2, 1, "e4m3") @ mxq(f64(V3), 0, "e4m3")) + f64(c3)
    return psi_state[:, None, :] + psi_adv - psi_adv.mean(axis=1, keepdims=True)


def e4m3fn_bytes(y):
    return np.clip(np.asarray(y, np.float64), -448.0, 448.0).astype(np.float32).astype(ml_dtypes.float8_e4m3fn).view(np.uint8)


def e4m3fn_values(b):
    return np.asarray(b, np.uint8).view(ml_dtypes.float8_e4m3fn).astype(np.float64)


def setup_inputs():
    d = draw0()
    x0 = np.asarray(d['h1']).astype(np.float64)
    s = (np.max(np.abs(x0), axis=(0, 1), keepdims=True) / 448.0).astype(np.float32)
    out = {}
    for k, v in d.items():
        if k == 'h1':
            out['h1_bytes'] = e4m3fn_bytes(x0 / s.astype(np.float64))
            out['h1_scale'] = s
        else:
            out[k] = v
    return out


def reference(h1_bytes, h1_scale, W2, b2, W3, b3, g1, V2, c2, V3, c3):
    return core(e4m3fn_values(h1_bytes) * h1_scale.astype(np.float64), W2, b2, W3, b3, g1, V2, c2, V3, c3)

@@ -1,0 +1,466 @@
+from contextlib import ExitStack
+
+import concourse.mybir as mybir
+from concourse.masks import make_identity
+
+B, A, F, S = 512, 16, 512, 256
+FLOPS = 2 * B * (A + 1) * (F * F + F * S)
+
+F32 = mybir.dt.float32
+BF16 = mybir.dt.bfloat16
+U32 = mybir.dt.uint32
+U8 = mybir.dt.uint8
+FP8 = mybir.dt.float8_e4m3fn
+FP8X4 = mybir.dt.float8_e4m3fn_x4
+ADD = mybir.AluOpType.add
+MAX = mybir.AluOpType.max
+MULT = mybir.AluOpType.mult
+RELU = mybir.ActivationFunctionType.Relu
+IDENT = mybir.ActivationFunctionType.Identity
+AXIS_X = mybir.AxisListType.X
+
+P = 128
+T = 4
+STATE = A
+GROUP = 4
+PHASES = ((0, 256), (256, 256))
+ORDER = (
+    ("load", -4),
+    ("turn", -1),
+    ("quant_x", 0),
+    ("quant_w2", 0),
+    ("quant_w3", 0),
+    ("turn_copy", -1),
+    ("w2_s", -1),
+    ("w3_s", -1),
+    ("h2_s", 1),
+    ("first_a", 0),
+    ("first_b", 0),
+    ("widen", -2),
+    ("quant_h2", 2),
+    ("second", 2),
+    ("w2_v", -1),
+    ("w3_v", -1),
+    ("h2_v", 1),
+    ("hidden_a", 0),
+    ("hidden_b", 0),
+    ("second_out", 2),
+    ("result_out", 1),
+    ("result", 0),
+)
+HA_V = (0, 0)
+HG_S = (256, 64)
+W2_S = 0
+W3_S = 64
+OC_S = ((9, 9), (9, 0), (9, 0))
+SO_V = (0, 0)
+OUT_EVERY = (1, 1)
+FAST = False
+BUFS = {"x_bytes": 3, "w2_raw": 3, "w3_raw": 3, "x_rows": 4, "x_grp": 3, "x_codes": 3, "x_scales": 3, "w2_grp": 2, "w3_grp": 2, "h2_planes": 3, "h2_grp": 2, "h2_codes": 3, "h2_scales": 3, "staged": 3}
+
+
+def tile_psicritic_pa_kernel(tc, h1_bytes, h1_scale, W2, b2, W3, b3, g1, V2, c2, V3, c3, out):
+    nc = tc.nc
+    units = [(ph, a) for ph in range(len(PHASES)) for a in [STATE] + list(range(A))]
+    n_units = len(units)
+
+    with ExitStack() as ctx:
+        keep = ctx.enter_context(tc.tile_pool(name="keep", bufs=1))
+        raw = ctx.enter_context(tc.tile_pool(name="raw", bufs=3))
+        work = ctx.enter_context(tc.tile_pool(name="work", bufs=3))
+        psum = ctx.enter_context(tc.psum_pool(name="psum", bufs=1))
+
+        def bank(name):
+            return psum.tile([P, 512], F32, name=name, tag="ring", bufs=6)
+
+        w2_codes = keep.tile([P, (A + 1) * F], U32, align_bytes=64, name="w2_codes")
+        w2_scales = keep.tile([P, (A + 1) * F], U8, align_bytes=64, name="w2_scales")
+        w3_codes = keep.tile([P, (A + 1) * S], U32, align_bytes=64, name="w3_codes")
+        w3_scales = keep.tile([P, (A + 1) * S], U8, align_bytes=64, name="w3_scales")
+        ident = keep.tile([P, P], F32, name="ident")
+        scale = keep.tile([P, 2, F], F32, align_bytes=64, name="scale")
+        b2_rows = keep.tile([P, F], BF16, name="b2_rows")
+        b3_rows = keep.tile([P, S], BF16, name="b3_rows")
+        b2_f32 = keep.tile([P, F], F32, name="b2_f32")
+        b3_f32 = keep.tile([P, S], F32, name="b3_f32")
+        b2_col = keep.tile([P, T, A + 1], F32, name="b2_col")
+        b3_col = keep.tile([P, 2, A + 1], F32, name="b3_col")
+        b3_sum = keep.tile([P, 2], F32, name="b3_sum")
+        state_bias = keep.tile([P, 2], F32, name="state_bias")
+        warm = keep.tile([P, 1], F32, name="warm")
+
+        x_bytes = {}
+        x_rows = {}
+        w2_raw = {}
+        w3_raw = {}
+        w2_grp = {}
+        w3_grp = {}
+        turned = {}
+        x_grp = {}
+        x_q = {}
+        hid_banks = {}
+        h2_planes = {}
+        h2_grp = {}
+        h2_q = {}
+        second = {}
+        state_t = {}
+        adv = {}
+        sums = {}
+        items = []
+        results = {}
+        staged = {}
+
+        def wt(shape, dtype, name):
+            return work.tile(shape, dtype, name=name, align_bytes=64, bufs=BUFS[name])
+
+        def interleave(engine_copy, dst, src):
+            if FAST:
+                engine_copy(
+                    out=dst.rearrange("p (c i) j -> p c j i", i=4),
+                    in_=src.rearrange("p j (c i) -> p c j i", i=4),
+                )
+            else:
+                engine_copy(out=dst, in_=src.rearrange("p j c -> p c j"))
+
+        def load(n):
+            ph, a = units[n]
+            t0, nt = PHASES[ph]
+            ni = nt // P
+            if a == STATE:
+                t = wt([P, ni, F], BF16, "x_rows")
+                nc.sync.dma_start(out=t[:], in_=g1[t0 : t0 + nt, :].rearrange("(i p) k -> p i k", p=P))
+                x_rows[n] = t
+            elif a % GROUP == 0:
+                t = raw.tile([P, GROUP, ni, F], U8, name="x_bytes", align_bytes=64, bufs=BUFS["x_bytes"])
+                for i in range(ni):
+                    rows = slice(t0 + i * P, t0 + (i + 1) * P)
+                    nc.sync.dma_start(out=t[:, :, i, :], in_=h1_bytes[rows, a : a + GROUP, :])
+                for j in range(GROUP):
+                    x_bytes[n + j] = (t, j)
+            if ph == 0:
+                src2 = V2 if a == STATE else W2[a]
+                src3 = V3 if a == STATE else W3[a]
+                t2 = raw.tile([P, T, F], BF16, name="w2_raw", align_bytes=64, bufs=BUFS["w2_raw"])
+                nc.sync.dma_start(out=t2[:], in_=src2.rearrange("(p j) c -> p j c", j=T))
+                t3 = raw.tile([P, T, S], BF16, name="w3_raw", align_bytes=64, bufs=BUFS["w3_raw"])
+                nc.sync.dma_start(out=t3[:], in_=src3.rearrange("(p j) c -> p j c", j=T))
+                w2_raw[a] = t2
+                w3_raw[a] = t3
+
+        def widen(n):
+            ph, a = units[n]
+            if a == STATE:
+                return
+            ni = PHASES[ph][1] // P
+            src, j = x_bytes[n]
+            t = wt([P, ni, F], BF16, "x_rows")
+            nc.vector.tensor_tensor(
+                out=t[:].rearrange("p i k -> p (i k)"),
+                in0=src[:, j, :, :].rearrange("p i k -> p (i k)").bitcast(FP8),
+                in1=scale[:, 0:ni, :].rearrange("p i k -> p (i k)"),
+                op=MULT,
+            )
+            x_rows[n] = t
+
+        def turn(n):
+            ph, a = units[n]
+            ni = PHASES[ph][1] // P
+            ps = bank("turned")
+            view = ps[:, 0 : ni * 256].rearrange("p (i u r) -> p i u r", i=ni, u=2)
+            for i in range(ni):
+                words = x_rows[n][:, i, :].bitcast(F32)
+                for u in range(2):
+                    nc.tensor.transpose(view[:, i, u, :], words[:, u:256:2], ident[:])
+            turned[n] = view
+
+        def turn_copy(n):
+            ph, a = units[n]
+            nt = PHASES[ph][1]
+            t = wt([P, nt * T], BF16, "x_grp")
+            nc.scalar.copy(
+                out=t[:].bitcast(F32).rearrange("p (i r u) -> p i r u", i=nt // P, u=2),
+                in_=turned[n].rearrange("p i u r -> p i r u"),
+            )
+            x_grp[n] = t
+
+        def quant_x(n):
+            ph, a = units[n]
+            nt = PHASES[ph][1]
+            codes = wt([P, nt], U32, "x_codes")
+            scales = wt([P, nt], U8, "x_scales")
+            nc.vector.quantize_mx(out=codes[:].bitcast(FP8X4), scales=scales[:], in_=x_grp[n][:])
+            x_q[n] = (codes, scales)
+
+        def quant_w2(n):
+            ph, a = units[n]
+            if ph == 0:
+                cols = slice(a * F, (a + 1) * F)
+                nc.vector.quantize_mx(out=w2_codes[:, cols].bitcast(FP8X4), scales=w2_scales[:, cols], in_=w2_grp[a][:])
+
+        def quant_w3(n):
+            ph, a = units[n]
+            if ph == 0:
+                cols = slice(a * S, (a + 1) * S)
+                nc.vector.quantize_mx(out=w3_codes[:, cols].bitcast(FP8X4), scales=w3_scales[:, cols], in_=w3_grp[a][:])
+
+        def group_w3_part(n, engine_copy, lo, hi):
+            ph, a = units[n]
+            if ph == 0 and lo < hi:
+                if a not in w3_grp:
+                    w3_grp[a] = wt([P, S * T], BF16, "w3_grp")
+                dst = w3_grp[a][:].rearrange("p (c j) -> p c j", j=T)[:, lo:hi, :]
+                interleave(engine_copy, dst, w3_raw[a][:, :, lo:hi])
+
+        def group_w3_s(n):
+            group_w3_part(n, nc.scalar.copy, 0, W3_S)
+
+        def group_w3_v(n):
+            group_w3_part(n, nc.vector.tensor_copy, W3_S, S)
+
+        def group_w2_part(n, engine_copy, lo, hi):
+            ph, a = units[n]
+            if ph == 0 and lo < hi:
+                if a not in w2_grp:
+                    w2_grp[a] = wt([P, F * T], BF16, "w2_grp")
+                engine_copy(
+                    out=w2_grp[a][:].rearrange("p (t m j) -> p t m j", t=T, j=T)[:, lo:hi],
+                    in_=w2_raw[a][:].rearrange("p j (m t) -> p t m j", t=T)[:, lo:hi],
+                )
+
+        def group_w2_s(n):
+            group_w2_part(n, nc.scalar.copy, 0, W2_S)
+
+        def group_w2_v(n):
+            group_w2_part(n, nc.vector.tensor_copy, W2_S, T)
+
+        def first_product(n, h):
+            ph, a = units[n]
+            nt = PHASES[ph][1]
+            codes, scales = x_q[n]
+            per_bank = 512 // nt
+            if h * per_bank >= T:
+                return
+            ps = bank("hidden")
+            for j in range(per_bank):
+                t = h * per_bank + j
+                view = ps[:, j * nt : (j + 1) * nt]
+                cols = slice(a * F + t * P, a * F + (t + 1) * P)
+                nc.tensor.matmul_mx(
+                    out=view,
+                    lhsT=w2_codes[:, cols].bitcast(FP8X4),
+                    lhsT_scale=w2_scales[:, cols],
+                    rhs=codes[:].bitcast(FP8X4),
+                    rhs_scale=scales[:],
+                    start=True,
+                    stop=True,
+                )
+                hid_banks[(n, t)] = view
+
+        def hidden(n, h):
+            ph, a = units[n]
+            nt = PHASES[ph][1]
+            per_bank = 512 // nt
+            if h * per_bank >= T:
+                return
+            if h == 0:
+                h2_planes[n] = wt([P, T, nt], BF16, "h2_planes")
+            for t in range(h * per_bank, (h + 1) * per_bank):
+                dst, src, bias = h2_planes[n][:, t, :], hid_banks[(n, t)], b2_col[:, t, a : a + 1]
+                if t >= T - HA_V[ph]:
+                    nc.vector.tensor_scalar(out=dst, in0=src, scalar1=bias, scalar2=0.0, op0=ADD, op1=MAX)
+                else:
+                    nc.scalar.activation(out=dst, in_=src, func=RELU, bias=bias, scale=1.0)
+
+        def group_h2_part(n, engine_copy, lo, hi):
+            ph, a = units[n]
+            nt = PHASES[ph][1]
+            if lo < hi:
+                if n not in h2_grp:
+                    h2_grp[n] = wt([P, nt * T], BF16, "h2_grp")
+                dst = h2_grp[n][:].rearrange("p (n j) -> p n j", j=T)[:, lo:hi, :]
+                interleave(engine_copy, dst, h2_planes[n][:, :, lo:hi])
+
+        def group_h2_s(n):
+            group_h2_part(n, nc.scalar.copy, 0, HG_S[units[n][0]])
+
+        def group_h2_v(n):
+            ph, a = units[n]
+            group_h2_part(n, nc.vector.tensor_copy, HG_S[ph], PHASES[ph][1])
+
+        def quant_h2(n):
+            ph, a = units[n]
+            nt = PHASES[ph][1]
+            codes = wt([P, nt], U32, "h2_codes")
+            scales = wt([P, nt], U8, "h2_scales")
+            nc.vector.quantize_mx(out=codes[:].bitcast(FP8X4), scales=scales[:], in_=h2_grp[n][:])
+            h2_q[n] = (codes, scales)
+
+        def second_product(n):
+            ph, a = units[n]
+            nt = PHASES[ph][1]
+            codes, scales = h2_q[n]
+            ps = bank("second")
+            second[n] = ps
+            if a == 0:
+                sums[ph] = [psum.tile([P, 512], F32, name="sum0"), psum.tile([P, 512], F32, name="sum1")]
+            for h in range(2):
+                cols = slice(a * S + h * P, a * S + (h + 1) * P)
+                targets = [(ps[:, h * nt : (h + 1) * nt], True, True)]
+                if a != STATE:
+                    targets.append((sums[ph][h][:, 0:nt], a == 0, a == A - 1))
+                for view, first, last in targets:
+                    nc.tensor.matmul_mx(
+                        out=view,
+                        lhsT=w3_codes[:, cols].bitcast(FP8X4),
+                        lhsT_scale=w3_scales[:, cols],
+                        rhs=codes[:].bitcast(FP8X4),
+                        rhs_scale=scales[:],
+                        start=first,
+                        stop=last,
+                    )
+
+        def second_out(n):
+            ph, a = units[n]
+            nt = PHASES[ph][1]
+            ps = second[n]
+            if a == STATE:
+                state_t[ph] = work.tile([P, 2, nt], F32, name="state_t", bufs=2)
+                adv[ph] = keep.tile([P, A, 2, nt], F32, name="adv%d" % (ph % 2))
+            for h in range(2):
+                if a == STATE:
+                    dst, bias = state_t[ph][:, h, :], state_bias[:, h : h + 1]
+                else:
+                    dst, bias = adv[ph][:, a, h, :], b3_col[:, h, a : a + 1]
+                src = ps[:, h * nt : (h + 1) * nt]
+                if h < SO_V[ph]:
+                    nc.vector.tensor_scalar(out=dst, in0=src, scalar1=bias, scalar2=None, op0=ADD)
+                else:
+                    nc.scalar.activation(out=dst, in_=src, func=IDENT, bias=bias, scale=1.0)
+            if a == A - 1:
+                common = work.tile([P, 2, nt], F32, name="common", bufs=2)
+                for h in range(2):
+                    nc.vector.scalar_tensor_tensor(
+                        out=common[:, h, :], in0=sums[ph][h][:, 0:nt], scalar=-1.0 / A, in1=state_t[ph][:, h, :],
+                        op0=MULT, op1=ADD,
+                    )
+                for i in range(nt // P):
+                    for pair in range(A // 2):
+                        items.append((ph, i, pair, common))
+
+        def result_tensor(k):
+            ph, i, pair, common = items[k]
+            toks = slice(i * P, (i + 1) * P)
+            ps = bank("result")
+            view = ps[:].rearrange("p (a h m) -> p a h m", a=2, h=2)
+            for j in range(2):
+                for h in range(2):
+                    nc.tensor.matmul(
+                        out=view[:, j, h, :], lhsT=adv[ph][:, 2 * pair + j, h, toks], rhs=ident[:],
+                        start=True, stop=False, is_transpose=True,
+                    )
+                    nc.tensor.matmul(
+                        out=view[:, j, h, :], lhsT=common[:, h, toks], rhs=ident[:],
+                        start=False, stop=True, is_transpose=True,
+                    )
+            results[k] = ps
+
+        def result_out(k):
+            ph, i, pair, common = items[k]
+            t0, nt = PHASES[ph]
+            if pair % 2 == 0:
+                staged[0] = work.tile([P, 4, S], F32, name="staged", bufs=BUFS["staged"])
+            half = slice((pair % 2) * 2, (pair % 2) * 2 + 2)
+            dst = staged[0][:, half, :].rearrange("p a s -> p (a s)")
+            last_phase = ph == len(PHASES) - 1
+            if (k % 2 == 0) if last_phase else (k % len(OC_S[ph + 1]) in OC_S[ph + 1]):
+                nc.scalar.copy(out=dst, in_=results[k][:])
+            else:
+                nc.vector.tensor_copy(out=dst, in_=results[k][:])
+            if pair % 2 == 1:
+                rows = slice(t0 + i * P, t0 + (i + 1) * P)
+                nc.sync.dma_start(out=out[rows, 2 * pair - 2 : 2 * pair + 2, :], in_=staged[0][:])
+
+        def setup():
+            nc.vector.memset(b2_rows[:], 0.0)
+            nc.vector.memset(b3_rows[:], 0.0)
+            nc.vector.memset(warm[:], 0.0)
+            nc.scalar.activation(out=warm[:], in_=warm[:], func=RELU, bias=0.0, scale=1.0)
+            make_identity(nc, ident[:])
+
+        def setup_loads():
+            nc.sync.dma_start(out=b2_rows[0:A, :], in_=b2)
+            nc.sync.dma_start(out=b2_rows[A : A + 1, :], in_=c2.rearrange("(o f) -> o f", o=1))
+            nc.sync.dma_start(out=b3_rows[0:A, :], in_=b3)
+            nc.sync.dma_start(out=b3_rows[A : A + 1, :], in_=c3.rearrange("(o f) -> o f", o=1))
+            nc.sync.dma_start(out=scale[:, 0, :], in_=h1_scale.rearrange("a b k -> (a b k)").partition_broadcast(P))
+
+        def setup_biases():
+            nc.vector.tensor_copy(out=b2_f32[:], in_=b2_rows[:])
+            nc.vector.tensor_copy(out=b3_f32[:], in_=b3_rows[:])
+            ps = bank("bias2")
+            view = ps[:].rearrange("p (t a) -> p t a", t=T)
+            for t in range(T):
+                nc.tensor.transpose(view[:, t, :], b2_f32[:, t:F:T], ident[:])
+            nc.vector.tensor_copy(out=b2_col[:], in_=view[:, :, 0 : A + 1])
+            ps3 = bank("bias3")
+            view3 = ps3[:, 0:256].rearrange("p (h a) -> p h a", h=2)
+            for h in range(2):
+                nc.tensor.transpose(view3[:, h, :], b3_f32[:, h * P : (h + 1) * P], ident[:])
+            nc.vector.tensor_copy(out=b3_col[:], in_=view3[:, :, 0 : A + 1])
+            nc.vector.reduce_sum(out=b3_sum[:], in_=b3_col[:, :, 0:A], axis=AXIS_X)
+            nc.vector.scalar_tensor_tensor(
+                out=state_bias[:], in0=b3_sum[:], scalar=-1.0 / A, in1=b3_col[:, :, A], op0=MULT, op1=ADD,
+            )
+
+        def first_a(n):
+            first_product(n, 0)
+
+        def first_b(n):
+            first_product(n, 1)
+
+        def hidden_a(n):
+            hidden(n, 0)
+
+        def hidden_b(n):
+            hidden(n, 1)
+
+        stages = {
+            "load": load, "widen": widen, "turn": turn, "turn_copy": turn_copy, "quant_x": quant_x,
+            "quant_w2": quant_w2, "quant_w3": quant_w3, "w2_s": group_w2_s, "w2_v": group_w2_v,
+            "w3_s": group_w3_s, "w3_v": group_w3_v, "first_a": first_a, "first_b": first_b,
+            "hidden_a": hidden_a, "hidden_b": hidden_b, "h2_s": group_h2_s, "h2_v": group_h2_v,
+            "quant_h2": quant_h2, "second": second_product, "second_out": second_out,
+        }
+        lag_min = min([lag for name, lag in ORDER])
+        lag_max = max([lag for name, lag in ORDER])
+        begun = 0
+        ended = 0
+        step = 0
+        setup()
+        for s in range(lag_min, n_units + lag_max + 1):
+            for name, lag in ORDER:
+                n = s - lag
+                if name == "result":
+                    ph = units[max(0, min(s, n_units - 1))][0]
+                    if begun < len(items) and s % OUT_EVERY[ph] == 0:
+                        result_tensor(begun)
+                        begun += 1
+                elif name == "result_out":
+                    if ended < begun and (lag == 0 or ended < step):
+                        result_out(ended)
+                        ended += 1
+                elif 0 <= n < n_units:
+                    stages[name](n)
+                if name == "load" and s == lag_min:
+                    setup_loads()
+                if name == "widen" and n == 0:
+                    setup_biases()
+                    nc.vector.tensor_copy(out=scale[:, 1, :], in_=scale[:, 0, :])
+            step = begun
+        while ended < len(items):
+            if begun < len(items) and begun < ended + 3:
+                result_tensor(begun)
+                begun += 1
+            else:
+                result_out(ended)
+                ended += 1

@@ -21,64 +21,81 @@ AXIS_X = mybir.AxisListType.X
 
 P = 128
 T = 4
+NI = B // P
 STATE = A
-GROUP = 4
-PHASES = ((0, 256), (256, 256))
+MANUAL = True
+KINDS = "LLLLLLLA"
 ORDER = (
-    ("load", -4),
-    ("turn", -1),
+    ("load_w3", -3),
+    ("turn_a", -1),
+    ("turn_b", -1),
+    ("second_a", 3),
+    ("w2_s", -2),
+    ("second_b", 3),
+    ("w3_s", -3),
+    ("quant_w2", -1),
     ("quant_x", 0),
-    ("quant_w2", 0),
-    ("quant_w3", 0),
-    ("turn_copy", -1),
-    ("w2_s", -1),
-    ("w3_s", -1),
+    ("load_w2", -4),
+    ("quant_w3", -1),
+    ("w2_v", -2),
+    ("tc_a", -1),
     ("h2_s", 1),
-    ("first_a", 0),
-    ("first_b", 0),
+    ("tc_b", -1),
     ("widen", -2),
+    ("first_0", 0),
+    ("load_x", -3),
     ("quant_h2", 2),
-    ("second", 2),
-    ("w2_v", -1),
-    ("w3_v", -1),
     ("h2_v", 1),
-    ("hidden_a", 0),
-    ("hidden_b", 0),
-    ("second_out", 2),
-    ("result_out", 1),
-    ("result", 0),
+    ("second_out", 3),
+    ("w3_v", -2),
+    ("hid_0", 0),
+    ("first_1", 0),
+    ("first_3", 0),
+    ("hid_1", 0),
+    ("first_2", 0),
+    ("hid_3", 0),
+    ("hid_2", 0),
 )
-HA_V = (0, 0)
-HG_S = (256, 64)
-W2_S = 0
-W3_S = 64
-OC_S = ((9, 9), (9, 0), (9, 0))
-SO_V = (0, 0)
-OUT_EVERY = (1, 1)
-FAST = False
-BUFS = {"x_bytes": 3, "w2_raw": 3, "w3_raw": 3, "x_rows": 4, "x_grp": 3, "x_codes": 3, "x_scales": 3, "w2_grp": 2, "w3_grp": 2, "h2_planes": 3, "h2_grp": 2, "h2_codes": 3, "h2_scales": 3, "staged": 3}
+HA_V = [[0],[1,1,0]]
+HG_S = [[64,384,448,320,256],[192,128,192,192,512]]
+W2_S = [[0,0,2,0,0],[0,0,0]]
+W3_S = [[0,256,256,256],[]]
+SO_V = [[0,2,1,2],[0,0,0,0]]
+AHEAD = 1
+LAG = 1
+FAST = True
+BUFS = {"x_bytes":3,"w2_raw":3,"w3_raw":2,"x_grp":3,"x_codes":2,"w2_codes":2,"w2_grp":2,"w3_grp":3,"h2_planes":2,"h2_grp":2,"h2_codes":2,"x_scales":2,"w2_scales":2,"x_rows":2,"staged":5}
 
 
 def tile_psicritic_pa_kernel(tc, h1_bytes, h1_scale, W2, b2, W3, b3, g1, V2, c2, V3, c3, out):
     nc = tc.nc
-    units = [(ph, a) for ph in range(len(PHASES)) for a in [STATE] + list(range(A))]
+    units = [STATE] + list(range(A))
     n_units = len(units)
+    n_late = 2 * KINDS.count("L")
+
+    def knob(values, n):
+        if n < len(values[0]) - 1:
+            return values[0][n]
+        back = n_units - 1 - n
+        if back < len(values[1]):
+            return values[1][back]
+        return values[0][-1]
 
     with ExitStack() as ctx:
         keep = ctx.enter_context(tc.tile_pool(name="keep", bufs=1))
         raw = ctx.enter_context(tc.tile_pool(name="raw", bufs=3))
         work = ctx.enter_context(tc.tile_pool(name="work", bufs=3))
         psum = ctx.enter_context(tc.psum_pool(name="psum", bufs=1))
+        if MANUAL:
+            ctx.enter_context(tc.manual_schedule())
 
         def bank(name):
             return psum.tile([P, 512], F32, name=name, tag="ring", bufs=6)
 
-        w2_codes = keep.tile([P, (A + 1) * F], U32, align_bytes=64, name="w2_codes")
-        w2_scales = keep.tile([P, (A + 1) * F], U8, align_bytes=64, name="w2_scales")
         w3_codes = keep.tile([P, (A + 1) * S], U32, align_bytes=64, name="w3_codes")
         w3_scales = keep.tile([P, (A + 1) * S], U8, align_bytes=64, name="w3_scales")
         ident = keep.tile([P, P], F32, name="ident")
-        scale = keep.tile([P, 2, F], F32, align_bytes=64, name="scale")
+        scale = keep.tile([P, NI, F], F32, align_bytes=64, name="scale")
         b2_rows = keep.tile([P, F], BF16, name="b2_rows")
         b3_rows = keep.tile([P, S], BF16, name="b3_rows")
         b2_f32 = keep.tile([P, F], F32, name="b2_f32")
@@ -87,7 +104,12 @@ def tile_psicritic_pa_kernel(tc, h1_bytes, h1_scale, W2, b2, W3, b3, g1, V2, c2,
         b3_col = keep.tile([P, 2, A + 1], F32, name="b3_col")
         b3_sum = keep.tile([P, 2], F32, name="b3_sum")
         state_bias = keep.tile([P, 2], F32, name="state_bias")
+        state_t = keep.tile([P, 2, B], F32, name="state_t")
+        common = keep.tile([P, 2, B], F32, name="common")
+        common_rows = keep.tile([P, NI, S], F32, name="common_rows")
+        b3_wide = keep.tile([P, A, S], BF16, name="b3_wide")
         warm = keep.tile([P, 1], F32, name="warm")
+        sums = [psum.tile([P, B], F32, name="sum0"), psum.tile([P, B], F32, name="sum1")]
 
         x_bytes = {}
         x_rows = {}
@@ -95,19 +117,19 @@ def tile_psicritic_pa_kernel(tc, h1_bytes, h1_scale, W2, b2, W3, b3, g1, V2, c2,
         w3_raw = {}
         w2_grp = {}
         w3_grp = {}
+        w2_q = {}
         turned = {}
         x_grp = {}
         x_q = {}
-        hid_banks = {}
+        hid = {}
         h2_planes = {}
         h2_grp = {}
         h2_q = {}
         second = {}
-        state_t = {}
         adv = {}
-        sums = {}
-        items = []
+        rows = {}
         results = {}
+        shared = {}
         staged = {}
 
         def wt(shape, dtype, name):
@@ -122,263 +144,254 @@ def tile_psicritic_pa_kernel(tc, h1_bytes, h1_scale, W2, b2, W3, b3, g1, V2, c2,
             else:
                 engine_copy(out=dst, in_=src.rearrange("p j c -> p c j"))
 
-        def load(n):
-            ph, a = units[n]
-            t0, nt = PHASES[ph]
-            ni = nt // P
+        def load_x(n):
+            a = units[n]
             if a == STATE:
-                t = wt([P, ni, F], BF16, "x_rows")
-                nc.sync.dma_start(out=t[:], in_=g1[t0 : t0 + nt, :].rearrange("(i p) k -> p i k", p=P))
+                t = wt([P, NI, F], BF16, "x_rows")
+                nc.sync.dma_start(out=t[:], in_=g1.rearrange("(i p) k -> p i k", p=P))
                 x_rows[n] = t
-            elif a % GROUP == 0:
-                t = raw.tile([P, GROUP, ni, F], U8, name="x_bytes", align_bytes=64, bufs=BUFS["x_bytes"])
-                for i in range(ni):
-                    rows = slice(t0 + i * P, t0 + (i + 1) * P)
-                    nc.sync.dma_start(out=t[:, :, i, :], in_=h1_bytes[rows, a : a + GROUP, :])
-                for j in range(GROUP):
-                    x_bytes[n + j] = (t, j)
-            if ph == 0:
-                src2 = V2 if a == STATE else W2[a]
-                src3 = V3 if a == STATE else W3[a]
-                t2 = raw.tile([P, T, F], BF16, name="w2_raw", align_bytes=64, bufs=BUFS["w2_raw"])
-                nc.sync.dma_start(out=t2[:], in_=src2.rearrange("(p j) c -> p j c", j=T))
-                t3 = raw.tile([P, T, S], BF16, name="w3_raw", align_bytes=64, bufs=BUFS["w3_raw"])
-                nc.sync.dma_start(out=t3[:], in_=src3.rearrange("(p j) c -> p j c", j=T))
-                w2_raw[a] = t2
-                w3_raw[a] = t3
+            else:
+                t = raw.tile([P, NI, F], U8, name="x_bytes", align_bytes=64, bufs=BUFS["x_bytes"])
+                nc.sync.dma_start(out=t[:], in_=h1_bytes[:, a, :].rearrange("(i p) k -> p i k", p=P))
+                x_bytes[n] = t
+
+        def load_w2(n):
+            a = units[n]
+            t = raw.tile([P, T, F], BF16, name="w2_raw", align_bytes=64, bufs=BUFS["w2_raw"])
+            nc.sync.dma_start(out=t[:], in_=(V2 if a == STATE else W2[a]).rearrange("(p j) c -> p j c", j=T))
+            w2_raw[n] = t
+
+        def load_w3(n):
+            a = units[n]
+            t = raw.tile([P, T, S], BF16, name="w3_raw", align_bytes=64, bufs=BUFS["w3_raw"])
+            nc.sync.dma_start(out=t[:], in_=(V3 if a == STATE else W3[a]).rearrange("(p j) c -> p j c", j=T))
+            w3_raw[n] = t
 
         def widen(n):
-            ph, a = units[n]
-            if a == STATE:
+            if units[n] == STATE:
                 return
-            ni = PHASES[ph][1] // P
-            src, j = x_bytes[n]
-            t = wt([P, ni, F], BF16, "x_rows")
+            t = wt([P, NI, F], BF16, "x_rows")
             nc.vector.tensor_tensor(
                 out=t[:].rearrange("p i k -> p (i k)"),
-                in0=src[:, j, :, :].rearrange("p i k -> p (i k)").bitcast(FP8),
-                in1=scale[:, 0:ni, :].rearrange("p i k -> p (i k)"),
+                in0=x_bytes[n][:].rearrange("p i k -> p (i k)").bitcast(FP8),
+                in1=scale[:].rearrange("p i k -> p (i k)"),
                 op=MULT,
             )
             x_rows[n] = t
 
-        def turn(n):
-            ph, a = units[n]
-            ni = PHASES[ph][1] // P
+        def turn(n, half):
             ps = bank("turned")
-            view = ps[:, 0 : ni * 256].rearrange("p (i u r) -> p i u r", i=ni, u=2)
-            for i in range(ni):
-                words = x_rows[n][:, i, :].bitcast(F32)
+            view = ps[:].rearrange("p (i u r) -> p i u r", i=2, u=2)
+            for i in range(2):
+                words = x_rows[n][:, 2 * half + i, :].bitcast(F32)
                 for u in range(2):
                     nc.tensor.transpose(view[:, i, u, :], words[:, u:256:2], ident[:])
-            turned[n] = view
+            turned[(n, half)] = view
 
-        def turn_copy(n):
-            ph, a = units[n]
-            nt = PHASES[ph][1]
-            t = wt([P, nt * T], BF16, "x_grp")
+        def turn_copy(n, half):
+            if half == 0:
+                x_grp[n] = wt([P, B * T], BF16, "x_grp")
             nc.scalar.copy(
-                out=t[:].bitcast(F32).rearrange("p (i r u) -> p i r u", i=nt // P, u=2),
-                in_=turned[n].rearrange("p i u r -> p i r u"),
+                out=x_grp[n][:, half * 1024 : (half + 1) * 1024].bitcast(F32).rearrange("p (i r u) -> p i r u", i=2, u=2),
+                in_=turned[(n, half)].rearrange("p i u r -> p i r u"),
             )
-            x_grp[n] = t
+
+        def quant(codes, scales, grouped):
+            nc.vector.quantize_mx(out=codes.bitcast(FP8X4), scales=scales, in_=grouped)
 
         def quant_x(n):
-            ph, a = units[n]
-            nt = PHASES[ph][1]
-            codes = wt([P, nt], U32, "x_codes")
-            scales = wt([P, nt], U8, "x_scales")
-            nc.vector.quantize_mx(out=codes[:].bitcast(FP8X4), scales=scales[:], in_=x_grp[n][:])
+            codes = wt([P, B], U32, "x_codes")
+            scales = wt([P, B], U8, "x_scales")
+            quant(codes[:], scales[:], x_grp[n][:])
             x_q[n] = (codes, scales)
 
         def quant_w2(n):
-            ph, a = units[n]
-            if ph == 0:
-                cols = slice(a * F, (a + 1) * F)
-                nc.vector.quantize_mx(out=w2_codes[:, cols].bitcast(FP8X4), scales=w2_scales[:, cols], in_=w2_grp[a][:])
+            codes = wt([P, F], U32, "w2_codes")
+            scales = wt([P, F], U8, "w2_scales")
+            quant(codes[:], scales[:], w2_grp[n][:])
+            w2_q[n] = (codes, scales)
 
         def quant_w3(n):
-            ph, a = units[n]
-            if ph == 0:
-                cols = slice(a * S, (a + 1) * S)
-                nc.vector.quantize_mx(out=w3_codes[:, cols].bitcast(FP8X4), scales=w3_scales[:, cols], in_=w3_grp[a][:])
+            cols = slice(n * S, (n + 1) * S)
+            quant(w3_codes[:, cols], w3_scales[:, cols], w3_grp[n][:])
 
         def group_w3_part(n, engine_copy, lo, hi):
-            ph, a = units[n]
-            if ph == 0 and lo < hi:
-                if a not in w3_grp:
-                    w3_grp[a] = wt([P, S * T], BF16, "w3_grp")
-                dst = w3_grp[a][:].rearrange("p (c j) -> p c j", j=T)[:, lo:hi, :]
-                interleave(engine_copy, dst, w3_raw[a][:, :, lo:hi])
+            if lo < hi:
+                if n not in w3_grp:
+                    w3_grp[n] = wt([P, S * T], BF16, "w3_grp")
+                dst = w3_grp[n][:].rearrange("p (c j) -> p c j", j=T)[:, lo:hi, :]
+                interleave(engine_copy, dst, w3_raw[n][:, :, lo:hi])
 
-        def group_w3_s(n):
-            group_w3_part(n, nc.scalar.copy, 0, W3_S)
+        def w3_s(n):
+            group_w3_part(n, nc.scalar.copy, 0, knob(W3_S, n))
 
-        def group_w3_v(n):
-            group_w3_part(n, nc.vector.tensor_copy, W3_S, S)
+        def w3_v(n):
+            group_w3_part(n, nc.vector.tensor_copy, knob(W3_S, n), S)
 
         def group_w2_part(n, engine_copy, lo, hi):
-            ph, a = units[n]
-            if ph == 0 and lo < hi:
-                if a not in w2_grp:
-                    w2_grp[a] = wt([P, F * T], BF16, "w2_grp")
+            if lo < hi:
+                if n not in w2_grp:
+                    w2_grp[n] = wt([P, F * T], BF16, "w2_grp")
                 engine_copy(
-                    out=w2_grp[a][:].rearrange("p (t m j) -> p t m j", t=T, j=T)[:, lo:hi],
-                    in_=w2_raw[a][:].rearrange("p j (m t) -> p t m j", t=T)[:, lo:hi],
+                    out=w2_grp[n][:].rearrange("p (t m j) -> p t m j", t=T, j=T)[:, lo:hi],
+                    in_=w2_raw[n][:].rearrange("p j (m t) -> p t m j", t=T)[:, lo:hi],
                 )
 
-        def group_w2_s(n):
-            group_w2_part(n, nc.scalar.copy, 0, W2_S)
+        def w2_s(n):
+            group_w2_part(n, nc.scalar.copy, 0, knob(W2_S, n))
 
-        def group_w2_v(n):
-            group_w2_part(n, nc.vector.tensor_copy, W2_S, T)
+        def w2_v(n):
+            group_w2_part(n, nc.vector.tensor_copy, knob(W2_S, n), T)
 
-        def first_product(n, h):
-            ph, a = units[n]
-            nt = PHASES[ph][1]
-            codes, scales = x_q[n]
-            per_bank = 512 // nt
-            if h * per_bank >= T:
-                return
+        def first(n, t):
+            x_codes, x_scales = x_q[n]
+            codes, scales = w2_q[n]
             ps = bank("hidden")
-            for j in range(per_bank):
-                t = h * per_bank + j
-                view = ps[:, j * nt : (j + 1) * nt]
-                cols = slice(a * F + t * P, a * F + (t + 1) * P)
-                nc.tensor.matmul_mx(
-                    out=view,
-                    lhsT=w2_codes[:, cols].bitcast(FP8X4),
-                    lhsT_scale=w2_scales[:, cols],
-                    rhs=codes[:].bitcast(FP8X4),
-                    rhs_scale=scales[:],
-                    start=True,
-                    stop=True,
-                )
-                hid_banks[(n, t)] = view
+            nc.tensor.matmul_mx(
+                out=ps[:],
+                lhsT=codes[:, t * P : (t + 1) * P].bitcast(FP8X4),
+                lhsT_scale=scales[:, t * P : (t + 1) * P],
+                rhs=x_codes[:].bitcast(FP8X4),
+                rhs_scale=x_scales[:],
+                start=True,
+                stop=True,
+            )
+            hid[(n, t)] = ps
 
-        def hidden(n, h):
-            ph, a = units[n]
-            nt = PHASES[ph][1]
-            per_bank = 512 // nt
-            if h * per_bank >= T:
-                return
-            if h == 0:
-                h2_planes[n] = wt([P, T, nt], BF16, "h2_planes")
-            for t in range(h * per_bank, (h + 1) * per_bank):
-                dst, src, bias = h2_planes[n][:, t, :], hid_banks[(n, t)], b2_col[:, t, a : a + 1]
-                if t >= T - HA_V[ph]:
-                    nc.vector.tensor_scalar(out=dst, in0=src, scalar1=bias, scalar2=0.0, op0=ADD, op1=MAX)
-                else:
-                    nc.scalar.activation(out=dst, in_=src, func=RELU, bias=bias, scale=1.0)
+        def hidden(n, t):
+            a = units[n]
+            if n not in h2_planes:
+                h2_planes[n] = wt([P, T, B], BF16, "h2_planes")
+            dst, bias = h2_planes[n][:, t, :], b2_col[:, t, a : a + 1]
+            if t >= T - knob(HA_V, n):
+                nc.vector.tensor_scalar(out=dst, in0=hid[(n, t)][:], scalar1=bias, scalar2=0.0, op0=ADD, op1=MAX)
+            else:
+                nc.scalar.activation(out=dst, in_=hid[(n, t)][:], func=RELU, bias=bias, scale=1.0)
 
         def group_h2_part(n, engine_copy, lo, hi):
-            ph, a = units[n]
-            nt = PHASES[ph][1]
             if lo < hi:
                 if n not in h2_grp:
-                    h2_grp[n] = wt([P, nt * T], BF16, "h2_grp")
+                    h2_grp[n] = wt([P, B * T], BF16, "h2_grp")
                 dst = h2_grp[n][:].rearrange("p (n j) -> p n j", j=T)[:, lo:hi, :]
                 interleave(engine_copy, dst, h2_planes[n][:, :, lo:hi])
 
-        def group_h2_s(n):
-            group_h2_part(n, nc.scalar.copy, 0, HG_S[units[n][0]])
+        def h2_s(n):
+            group_h2_part(n, nc.scalar.copy, 0, knob(HG_S, n))
 
-        def group_h2_v(n):
-            ph, a = units[n]
-            group_h2_part(n, nc.vector.tensor_copy, HG_S[ph], PHASES[ph][1])
+        def h2_v(n):
+            group_h2_part(n, nc.vector.tensor_copy, knob(HG_S, n), B)
+
+        def kind(n):
+            return "A" if units[n] == STATE else KINDS[units[n] // 2]
 
         def quant_h2(n):
-            ph, a = units[n]
-            nt = PHASES[ph][1]
-            codes = wt([P, nt], U32, "h2_codes")
-            scales = wt([P, nt], U8, "h2_scales")
-            nc.vector.quantize_mx(out=codes[:].bitcast(FP8X4), scales=scales[:], in_=h2_grp[n][:])
+            late = kind(n) == "L"
+            name = "late" if late else "h2"
+            codes = work.tile([P, B], U32, name=name + "_codes", align_bytes=64, bufs=n_late if late else BUFS["h2_codes"])
+            scales = work.tile([P, B], U8, name=name + "_scales", align_bytes=64, bufs=n_late if late else BUFS["h2_codes"])
+            quant(codes[:], scales[:], h2_grp[n][:])
             h2_q[n] = (codes, scales)
 
-        def second_product(n):
-            ph, a = units[n]
-            nt = PHASES[ph][1]
+        def product2(view, n, h, start, stop):
             codes, scales = h2_q[n]
+            cols = slice(n * S + h * P, n * S + (h + 1) * P)
+            nc.tensor.matmul_mx(
+                out=view,
+                lhsT=w3_codes[:, cols].bitcast(FP8X4),
+                lhsT_scale=w3_scales[:, cols],
+                rhs=codes[:].bitcast(FP8X4),
+                rhs_scale=scales[:],
+                start=start,
+                stop=stop,
+            )
+
+        def summed(n, h):
+            a = units[n]
+            if a != STATE:
+                product2(sums[h][:], n, h, a == 0, a == A - 1)
+
+        def own(n, h):
             ps = bank("second")
-            second[n] = ps
-            if a == 0:
-                sums[ph] = [psum.tile([P, 512], F32, name="sum0"), psum.tile([P, 512], F32, name="sum1")]
-            for h in range(2):
-                cols = slice(a * S + h * P, a * S + (h + 1) * P)
-                targets = [(ps[:, h * nt : (h + 1) * nt], True, True)]
-                if a != STATE:
-                    targets.append((sums[ph][h][:, 0:nt], a == 0, a == A - 1))
-                for view, first, last in targets:
+            second[(n, h)] = ps
+            if kind(n) == "R":
+                codes, scales = h2_q[n]
+                cols = slice(n * S, (n + 1) * S)
+                for i in range(2):
+                    toks = slice((2 * h + i) * P, (2 * h + i + 1) * P)
                     nc.tensor.matmul_mx(
-                        out=view,
-                        lhsT=w3_codes[:, cols].bitcast(FP8X4),
-                        lhsT_scale=w3_scales[:, cols],
-                        rhs=codes[:].bitcast(FP8X4),
-                        rhs_scale=scales[:],
-                        start=first,
-                        stop=last,
+                        out=ps[:, i * S : (i + 1) * S],
+                        lhsT=codes[:, toks].bitcast(FP8X4),
+                        lhsT_scale=scales[:, toks],
+                        rhs=w3_codes[:, cols].bitcast(FP8X4),
+                        rhs_scale=w3_scales[:, cols],
+                        start=True,
+                        stop=True,
                     )
+            else:
+                product2(ps[:], n, h, True, True)
+
+        def own_out(n, h):
+            a = units[n]
+            ps = second[(n, h)]
+            if kind(n) == "R":
+                if a % 2 == 0 and h == 0:
+                    rows[a // 2] = keep.tile([P, 2, NI, S], F32, name="rows%d" % a)
+                nc.vector.tensor_tensor(
+                    out=rows[a // 2][:, a % 2, 2 * h : 2 * h + 2, :],
+                    in0=ps[:].rearrange("p (i s) -> p i s", i=2),
+                    in1=b3_wide[:, a : a + 1, :].to_broadcast([P, 2, S]),
+                    op=ADD,
+                )
+                return
+            if a == STATE:
+                dst, bias = state_t[:, h, :], state_bias[:, h : h + 1]
+            else:
+                if h == 0:
+                    if kind(n) == "A":
+                        adv[a] = keep.tile([P, 2, B], F32, name="adv%d" % a)
+                    else:
+                        adv[a] = work.tile([P, 2, B], F32, name="late_adv", bufs=min(n_late, 6))
+                dst, bias = adv[a][:, h, :], b3_col[:, h, a : a + 1]
+            if kind(n) == "A" and h < knob(SO_V, n):
+                nc.vector.tensor_scalar(out=dst, in0=ps[:], scalar1=bias, scalar2=None, op0=ADD)
+            else:
+                nc.scalar.activation(out=dst, in_=ps[:], func=IDENT, bias=bias, scale=1.0)
+
+        def second_a(n):
+            summed(n, 0)
+            if kind(n) != "L":
+                own(n, 0)
+
+        def second_b(n):
+            summed(n, 1)
+            if kind(n) != "L":
+                own(n, 1)
 
         def second_out(n):
-            ph, a = units[n]
-            nt = PHASES[ph][1]
-            ps = second[n]
-            if a == STATE:
-                state_t[ph] = work.tile([P, 2, nt], F32, name="state_t", bufs=2)
-                adv[ph] = keep.tile([P, A, 2, nt], F32, name="adv%d" % (ph % 2))
-            for h in range(2):
-                if a == STATE:
-                    dst, bias = state_t[ph][:, h, :], state_bias[:, h : h + 1]
-                else:
-                    dst, bias = adv[ph][:, a, h, :], b3_col[:, h, a : a + 1]
-                src = ps[:, h * nt : (h + 1) * nt]
-                if h < SO_V[ph]:
-                    nc.vector.tensor_scalar(out=dst, in0=src, scalar1=bias, scalar2=None, op0=ADD)
-                else:
-                    nc.scalar.activation(out=dst, in_=src, func=IDENT, bias=bias, scale=1.0)
-            if a == A - 1:
-                common = work.tile([P, 2, nt], F32, name="common", bufs=2)
-                for h in range(2):
-                    nc.vector.scalar_tensor_tensor(
-                        out=common[:, h, :], in0=sums[ph][h][:, 0:nt], scalar=-1.0 / A, in1=state_t[ph][:, h, :],
-                        op0=MULT, op1=ADD,
-                    )
-                for i in range(nt // P):
-                    for pair in range(A // 2):
-                        items.append((ph, i, pair, common))
+            if kind(n) != "L":
+                own_out(n, 0)
+                own_out(n, 1)
 
-        def result_tensor(k):
-            ph, i, pair, common = items[k]
+        def result_tensor(item):
+            e, i = item
             toks = slice(i * P, (i + 1) * P)
             ps = bank("result")
             view = ps[:].rearrange("p (a h m) -> p a h m", a=2, h=2)
             for j in range(2):
                 for h in range(2):
-                    nc.tensor.matmul(
-                        out=view[:, j, h, :], lhsT=adv[ph][:, 2 * pair + j, h, toks], rhs=ident[:],
-                        start=True, stop=False, is_transpose=True,
-                    )
-                    nc.tensor.matmul(
-                        out=view[:, j, h, :], lhsT=common[:, h, toks], rhs=ident[:],
-                        start=False, stop=True, is_transpose=True,
-                    )
-            results[k] = ps
+                    nc.tensor.transpose(view[:, j, h, :], adv[2 * e + j][:, h, toks], ident[:])
+            results[item] = ps[:].rearrange("p (a s) -> p a s", a=2)
 
-        def result_out(k):
-            ph, i, pair, common = items[k]
-            t0, nt = PHASES[ph]
-            if pair % 2 == 0:
-                staged[0] = work.tile([P, 4, S], F32, name="staged", bufs=BUFS["staged"])
-            half = slice((pair % 2) * 2, (pair % 2) * 2 + 2)
-            dst = staged[0][:, half, :].rearrange("p a s -> p (a s)")
-            last_phase = ph == len(PHASES) - 1
-            if (k % 2 == 0) if last_phase else (k % len(OC_S[ph + 1]) in OC_S[ph + 1]):
-                nc.scalar.copy(out=dst, in_=results[k][:])
-            else:
-                nc.vector.tensor_copy(out=dst, in_=results[k][:])
-            if pair % 2 == 1:
-                rows = slice(t0 + i * P, t0 + (i + 1) * P)
-                nc.sync.dma_start(out=out[rows, 2 * pair - 2 : 2 * pair + 2, :], in_=staged[0][:])
+        def result_out(item):
+            e, i = item
+            dst = work.tile([P, 2, S], F32, name="staged", bufs=BUFS["staged"])
+            nc.vector.tensor_tensor(
+                out=dst[:],
+                in0=rows[e][:, :, i, :] if KINDS[e] == "R" else results[item],
+                in1=common_rows[:, i : i + 1, :].to_broadcast([P, 2, S]),
+                op=ADD,
+            )
+            nc.sync.dma_start(out=out[i * P : (i + 1) * P, 2 * e : 2 * e + 2, :], in_=dst[:])
 
         def setup():
             nc.vector.memset(b2_rows[:], 0.0)
@@ -394,6 +407,13 @@ def tile_psicritic_pa_kernel(tc, h1_bytes, h1_scale, W2, b2, W3, b3, g1, V2, c2,
             nc.sync.dma_start(out=b3_rows[A : A + 1, :], in_=c3.rearrange("(o f) -> o f", o=1))
             nc.sync.dma_start(out=scale[:, 0, :], in_=h1_scale.rearrange("a b k -> (a b k)").partition_broadcast(P))
 
+        def row_bias_load():
+            nc.sync.dma_start(out=b3_wide[:].rearrange("p a s -> p (a s)"), in_=b3.rearrange("a s -> (a s)").partition_broadcast(P))
+
+        def setup_scale():
+            for i in range(1, NI):
+                nc.scalar.copy(out=scale[:, i, :], in_=scale[:, 0, :])
+
         def setup_biases():
             nc.vector.tensor_copy(out=b2_f32[:], in_=b2_rows[:])
             nc.vector.tensor_copy(out=b3_f32[:], in_=b3_rows[:])
@@ -401,66 +421,86 @@ def tile_psicritic_pa_kernel(tc, h1_bytes, h1_scale, W2, b2, W3, b3, g1, V2, c2,
             view = ps[:].rearrange("p (t a) -> p t a", t=T)
             for t in range(T):
                 nc.tensor.transpose(view[:, t, :], b2_f32[:, t:F:T], ident[:])
-            nc.vector.tensor_copy(out=b2_col[:], in_=view[:, :, 0 : A + 1])
             ps3 = bank("bias3")
             view3 = ps3[:, 0:256].rearrange("p (h a) -> p h a", h=2)
             for h in range(2):
                 nc.tensor.transpose(view3[:, h, :], b3_f32[:, h * P : (h + 1) * P], ident[:])
+            nc.vector.tensor_copy(out=b2_col[:], in_=view[:, :, 0 : A + 1])
             nc.vector.tensor_copy(out=b3_col[:], in_=view3[:, :, 0 : A + 1])
             nc.vector.reduce_sum(out=b3_sum[:], in_=b3_col[:, :, 0:A], axis=AXIS_X)
             nc.vector.scalar_tensor_tensor(
                 out=state_bias[:], in0=b3_sum[:], scalar=-1.0 / A, in1=b3_col[:, :, A], op0=MULT, op1=ADD,
             )
 
-        def first_a(n):
-            first_product(n, 0)
-
-        def first_b(n):
-            first_product(n, 1)
-
-        def hidden_a(n):
-            hidden(n, 0)
-
-        def hidden_b(n):
-            hidden(n, 1)
-
         stages = {
-            "load": load, "widen": widen, "turn": turn, "turn_copy": turn_copy, "quant_x": quant_x,
-            "quant_w2": quant_w2, "quant_w3": quant_w3, "w2_s": group_w2_s, "w2_v": group_w2_v,
-            "w3_s": group_w3_s, "w3_v": group_w3_v, "first_a": first_a, "first_b": first_b,
-            "hidden_a": hidden_a, "hidden_b": hidden_b, "h2_s": group_h2_s, "h2_v": group_h2_v,
-            "quant_h2": quant_h2, "second": second_product, "second_out": second_out,
+            "load_x": load_x, "load_w2": load_w2, "load_w3": load_w3, "widen": widen,
+            "turn_a": lambda n: turn(n, 0), "turn_b": lambda n: turn(n, 1),
+            "tc_a": lambda n: turn_copy(n, 0), "tc_b": lambda n: turn_copy(n, 1),
+            "quant_x": quant_x, "quant_w2": quant_w2, "quant_w3": quant_w3,
+            "w2_s": w2_s, "w2_v": w2_v, "w3_s": w3_s, "w3_v": w3_v,
+            "first_0": lambda n: first(n, 0), "first_1": lambda n: first(n, 1),
+            "first_2": lambda n: first(n, 2), "first_3": lambda n: first(n, 3),
+            "hid_0": lambda n: hidden(n, 0), "hid_1": lambda n: hidden(n, 1),
+            "hid_2": lambda n: hidden(n, 2), "hid_3": lambda n: hidden(n, 3),
+            "h2_s": h2_s, "h2_v": h2_v, "quant_h2": quant_h2,
+            "second_a": second_a, "second_b": second_b, "second_out": second_out,
         }
         lag_min = min([lag for name, lag in ORDER])
         lag_max = max([lag for name, lag in ORDER])
+        setup()
+        for s in range(lag_min, n_units + lag_max):
+            if s == 0:
+                setup_biases()
+            order = ORDER if s >= 0 else sorted(ORDER, key=lambda e: s - e[1])
+            for name, lag in order:
+                n = s - lag
+                if 0 <= n < n_units:
+                    stages[name](n)
+                if name == "load_w2" and n == 0:
+                    setup_loads()
+                    setup_scale()
+                if name == "load_w3" and n == 2 and "R" in KINDS:
+                    row_bias_load()
+
+        late = [n for n in range(n_units) if kind(n) == "L"]
+        turned_items = [(e, i) for k in "AL" for e in range(A // 2) if KINDS[e] == k for i in range(NI)]
+        row_items = [(e, i) for e in range(A // 2) if KINDS[e] == "R" for i in range(NI)]
+        owned = 0
+
+        def next_late():
+            own(late[owned], 0)
+            own(late[owned], 1)
+            own_out(late[owned], 0)
+            own_out(late[owned], 1)
+
+        while owned < min(AHEAD, len(late)):
+            next_late()
+            owned += 1
+        for h in range(2):
+            nc.vector.scalar_tensor_tensor(
+                out=common[:, h, :], in0=sums[h][:], scalar=-1.0 / A, in1=state_t[:, h, :], op0=MULT, op1=ADD,
+            )
+        for i in range(0, NI, 2):
+            ps = bank("shared_ps")
+            view = ps[:].rearrange("p (i h m) -> p i h m", i=2, h=2)
+            for j in range(2):
+                for h in range(2):
+                    nc.tensor.transpose(view[:, j, h, :], common[:, h, (i + j) * P : (i + j + 1) * P], ident[:])
+            nc.vector.tensor_copy(out=common_rows[:, i : i + 2, :].rearrange("p i s -> p (i s)"), in_=ps[:])
         begun = 0
         ended = 0
-        step = 0
-        setup()
-        for s in range(lag_min, n_units + lag_max + 1):
-            for name, lag in ORDER:
-                n = s - lag
-                if name == "result":
-                    ph = units[max(0, min(s, n_units - 1))][0]
-                    if begun < len(items) and s % OUT_EVERY[ph] == 0:
-                        result_tensor(begun)
-                        begun += 1
-                elif name == "result_out":
-                    if ended < begun and (lag == 0 or ended < step):
-                        result_out(ended)
-                        ended += 1
-                elif 0 <= n < n_units:
-                    stages[name](n)
-                if name == "load" and s == lag_min:
-                    setup_loads()
-                if name == "widen" and n == 0:
-                    setup_biases()
-                    nc.vector.tensor_copy(out=scale[:, 1, :], in_=scale[:, 0, :])
-            step = begun
-        while ended < len(items):
-            if begun < len(items) and begun < ended + 3:
-                result_tensor(begun)
+        row = 0
+        n_turned, n_row = len(turned_items), len(row_items)
+        while ended < n_turned or row < n_row:
+            while owned < len(late) and 2 * owned < begun + AHEAD * 2:
+                next_late()
+                owned += 1
+            while begun < min(n_turned, ended + 1 + LAG):
+                result_tensor(turned_items[begun])
                 begun += 1
-            else:
-                result_out(ended)
+            while row < n_row and (row * n_turned <= ended * n_row or ended == n_turned):
+                result_out(row_items[row])
+                row += 1
+            if ended < n_turned:
+                result_out(turned_items[ended])
                 ended += 1

@@ -24,54 +24,56 @@ T = 4
 NI = B // P
 STATE = A
 MANUAL = True
-KINDS = "LLLLLLLA"
+KINDS = "RLLLLLAL"
 ORDER = (
-    ("load_w3", -3),
-    ("turn_a", -1),
-    ("turn_b", -1),
-    ("second_a", 3),
-    ("w2_s", -2),
-    ("second_b", 3),
-    ("w3_s", -3),
-    ("quant_w2", -1),
     ("quant_x", 0),
-    ("load_w2", -4),
-    ("quant_w3", -1),
-    ("w2_v", -2),
+    ("quant_w3", 3),
+    ("h2_s", 2),
+    ("turn_b", -1),
+    ("w2", -2),
     ("tc_a", -1),
-    ("h2_s", 1),
-    ("tc_b", -1),
-    ("widen", -2),
-    ("first_0", 0),
-    ("load_x", -3),
-    ("quant_h2", 2),
-    ("h2_v", 1),
-    ("second_out", 3),
-    ("w3_v", -2),
-    ("hid_0", 0),
-    ("first_1", 0),
     ("first_3", 0),
-    ("hid_1", 0),
+    ("second_out", 5),
+    ("widen", -2),
     ("first_2", 0),
-    ("hid_3", 0),
+    ("load_w3", -2),
+    ("first_0", 0),
+    ("first_1", 0),
+    ("w3_v", 1),
+    ("second_b", 4),
+    ("quant_w2", -1),
+    ("w3_s", -2),
+    ("tc_b", -1),
+    ("turn_a", -2),
+    ("h2_v", 2),
     ("hid_2", 0),
+    ("load_x", -3),
+    ("hid_0", 0),
+    ("load_w2", -4),
+    ("quant_h2", 3),
+    ("hid_3", 0),
+    ("hid_1", 0),
+    ("second_a", 4),
 )
-HA_V = [[0],[1,1,0]]
-HG_S = [[64,384,448,320,256],[192,128,192,192,512]]
-W2_S = [[0,0,2,0,0],[0,0,0]]
-W3_S = [[0,256,256,256],[]]
-SO_V = [[0,2,1,2],[0,0,0,0]]
-AHEAD = 1
-LAG = 1
+HA_V = [[0,0,0,0,0],[0]]
+HG_S = [[192,256,64,384,352],[192,128,128,256]]
+W3_S = [[256],[128,192,64,192]]
+SO_V = [[0,0,2,1],[1,1,0,0]]
+AHEAD = 3
+RUN = 4
+GROUP = 2
+CROWS = 1
+RES = [0,1,2,2]
+SPLIT = 2
 FAST = True
-BUFS = {"x_bytes":3,"w2_raw":3,"w3_raw":2,"x_grp":3,"x_codes":2,"w2_codes":2,"w2_grp":2,"w3_grp":3,"h2_planes":2,"h2_grp":2,"h2_codes":2,"x_scales":2,"w2_scales":2,"x_rows":2,"staged":5}
+BUFS = {"x_bytes":2,"w2_raw":2,"w3_raw":4,"x_grp":2,"x_codes":2,"w2_codes":2,"w2_grp":2,"w3_grp":5,"h2_planes":3,"h2_grp":3,"h2_codes":3,"x_scales":2,"w2_scales":2,"x_rows":2,"staged":7}
 
 
 def tile_psicritic_pa_kernel(tc, h1_bytes, h1_scale, W2, b2, W3, b3, g1, V2, c2, V3, c3, out):
     nc = tc.nc
     units = [STATE] + list(range(A))
     n_units = len(units)
-    n_late = 2 * KINDS.count("L")
+    n_late = 2 * (KINDS.count("L") + KINDS.count("Q"))
 
     def knob(values, n):
         if n < len(values[0]) - 1:
@@ -107,7 +109,6 @@ def tile_psicritic_pa_kernel(tc, h1_bytes, h1_scale, W2, b2, W3, b3, g1, V2, c2,
         state_t = keep.tile([P, 2, B], F32, name="state_t")
         common = keep.tile([P, 2, B], F32, name="common")
         common_rows = keep.tile([P, NI, S], F32, name="common_rows")
-        b3_wide = keep.tile([P, A, S], BF16, name="b3_wide")
         warm = keep.tile([P, 1], F32, name="warm")
         sums = [psum.tile([P, B], F32, name="sum0"), psum.tile([P, B], F32, name="sum1")]
 
@@ -128,6 +129,8 @@ def tile_psicritic_pa_kernel(tc, h1_bytes, h1_scale, W2, b2, W3, b3, g1, V2, c2,
         second = {}
         adv = {}
         rows = {}
+        b3_wide = {}
+        bias_ps = {}
         results = {}
         shared = {}
         staged = {}
@@ -228,20 +231,12 @@ def tile_psicritic_pa_kernel(tc, h1_bytes, h1_scale, W2, b2, W3, b3, g1, V2, c2,
         def w3_v(n):
             group_w3_part(n, nc.vector.tensor_copy, knob(W3_S, n), S)
 
-        def group_w2_part(n, engine_copy, lo, hi):
-            if lo < hi:
-                if n not in w2_grp:
-                    w2_grp[n] = wt([P, F * T], BF16, "w2_grp")
-                engine_copy(
-                    out=w2_grp[n][:].rearrange("p (t m j) -> p t m j", t=T, j=T)[:, lo:hi],
-                    in_=w2_raw[n][:].rearrange("p j (m t) -> p t m j", t=T)[:, lo:hi],
-                )
-
-        def w2_s(n):
-            group_w2_part(n, nc.scalar.copy, 0, knob(W2_S, n))
-
-        def w2_v(n):
-            group_w2_part(n, nc.vector.tensor_copy, knob(W2_S, n), T)
+        def group_w2(n):
+            w2_grp[n] = wt([P, F * T], BF16, "w2_grp")
+            nc.vector.tensor_copy(
+                out=w2_grp[n][:].rearrange("p (t v m j) -> p v t j m", t=T, m=2, j=T),
+                in_=w2_raw[n][:].rearrange("p j (v m t) -> p v t j m", m=2, t=T),
+            )
 
         def first(n, t):
             x_codes, x_scales = x_q[n]
@@ -285,7 +280,7 @@ def tile_psicritic_pa_kernel(tc, h1_bytes, h1_scale, W2, b2, W3, b3, g1, V2, c2,
             return "A" if units[n] == STATE else KINDS[units[n] // 2]
 
         def quant_h2(n):
-            late = kind(n) == "L"
+            late = kind(n) in "LQ"
             name = "late" if late else "h2"
             codes = work.tile([P, B], U32, name=name + "_codes", align_bytes=64, bufs=n_late if late else BUFS["h2_codes"])
             scales = work.tile([P, B], U8, name=name + "_scales", align_bytes=64, bufs=n_late if late else BUFS["h2_codes"])
@@ -313,7 +308,7 @@ def tile_psicritic_pa_kernel(tc, h1_bytes, h1_scale, W2, b2, W3, b3, g1, V2, c2,
         def own(n, h):
             ps = bank("second")
             second[(n, h)] = ps
-            if kind(n) == "R":
+            if kind(n) in "RQ":
                 codes, scales = h2_q[n]
                 cols = slice(n * S, (n + 1) * S)
                 for i in range(2):
@@ -333,13 +328,13 @@ def tile_psicritic_pa_kernel(tc, h1_bytes, h1_scale, W2, b2, W3, b3, g1, V2, c2,
         def own_out(n, h):
             a = units[n]
             ps = second[(n, h)]
-            if kind(n) == "R":
+            if kind(n) in "RQ":
                 if a % 2 == 0 and h == 0:
                     rows[a // 2] = keep.tile([P, 2, NI, S], F32, name="rows%d" % a)
                 nc.vector.tensor_tensor(
                     out=rows[a // 2][:, a % 2, 2 * h : 2 * h + 2, :],
                     in0=ps[:].rearrange("p (i s) -> p i s", i=2),
-                    in1=b3_wide[:, a : a + 1, :].to_broadcast([P, 2, S]),
+                    in1=b3_wide[a // 2][:, a % 2 : a % 2 + 1, :].to_broadcast([P, 2, S]),
                     op=ADD,
                 )
                 return
@@ -359,23 +354,27 @@ def tile_psicritic_pa_kernel(tc, h1_bytes, h1_scale, W2, b2, W3, b3, g1, V2, c2,
 
         def second_a(n):
             summed(n, 0)
-            if kind(n) != "L":
+            if kind(n) not in "LQ":
                 own(n, 0)
 
         def second_b(n):
             summed(n, 1)
-            if kind(n) != "L":
+            if kind(n) not in "LQ":
                 own(n, 1)
 
         def second_out(n):
-            if kind(n) != "L":
+            if kind(n) not in "LQ":
                 own_out(n, 0)
                 own_out(n, 1)
 
         def result_tensor(item):
             e, i = item
             toks = slice(i * P, (i + 1) * P)
-            ps = bank("result")
+            where = RES[len(results) % len(RES)]
+            if where == 2:
+                ps = bank("result")
+            else:
+                ps = psum.tile([P, B], F32, name="sum%d" % where)
             view = ps[:].rearrange("p (a h m) -> p a h m", a=2, h=2)
             for j in range(2):
                 for h in range(2):
@@ -387,7 +386,7 @@ def tile_psicritic_pa_kernel(tc, h1_bytes, h1_scale, W2, b2, W3, b3, g1, V2, c2,
             dst = work.tile([P, 2, S], F32, name="staged", bufs=BUFS["staged"])
             nc.vector.tensor_tensor(
                 out=dst[:],
-                in0=rows[e][:, :, i, :] if KINDS[e] == "R" else results[item],
+                in0=rows[e][:, :, i, :] if KINDS[e] in "RQ" else results[item],
                 in1=common_rows[:, i : i + 1, :].to_broadcast([P, 2, S]),
                 op=ADD,
             )
@@ -408,7 +407,13 @@ def tile_psicritic_pa_kernel(tc, h1_bytes, h1_scale, W2, b2, W3, b3, g1, V2, c2,
             nc.sync.dma_start(out=scale[:, 0, :], in_=h1_scale.rearrange("a b k -> (a b k)").partition_broadcast(P))
 
         def row_bias_load():
-            nc.sync.dma_start(out=b3_wide[:].rearrange("p a s -> p (a s)"), in_=b3.rearrange("a s -> (a s)").partition_broadcast(P))
+            for e in range(A // 2):
+                if KINDS[e] in "RQ":
+                    b3_wide[e] = keep.tile([P, 2, S], BF16, name="b3_wide%d" % e)
+                    nc.sync.dma_start(
+                        out=b3_wide[e][:].rearrange("p a s -> p (a s)"),
+                        in_=b3[2 * e : 2 * e + 2, :].rearrange("a s -> (a s)").partition_broadcast(P),
+                    )
 
         def setup_scale():
             for i in range(1, NI):
@@ -425,6 +430,10 @@ def tile_psicritic_pa_kernel(tc, h1_bytes, h1_scale, W2, b2, W3, b3, g1, V2, c2,
             view3 = ps3[:, 0:256].rearrange("p (h a) -> p h a", h=2)
             for h in range(2):
                 nc.tensor.transpose(view3[:, h, :], b3_f32[:, h * P : (h + 1) * P], ident[:])
+            bias_ps[0] = (view, view3)
+
+        def bias_columns():
+            view, view3 = bias_ps[0]
             nc.vector.tensor_copy(out=b2_col[:], in_=view[:, :, 0 : A + 1])
             nc.vector.tensor_copy(out=b3_col[:], in_=view3[:, :, 0 : A + 1])
             nc.vector.reduce_sum(out=b3_sum[:], in_=b3_col[:, :, 0:A], axis=AXIS_X)
@@ -437,7 +446,7 @@ def tile_psicritic_pa_kernel(tc, h1_bytes, h1_scale, W2, b2, W3, b3, g1, V2, c2,
             "turn_a": lambda n: turn(n, 0), "turn_b": lambda n: turn(n, 1),
             "tc_a": lambda n: turn_copy(n, 0), "tc_b": lambda n: turn_copy(n, 1),
             "quant_x": quant_x, "quant_w2": quant_w2, "quant_w3": quant_w3,
-            "w2_s": w2_s, "w2_v": w2_v, "w3_s": w3_s, "w3_v": w3_v,
+            "w2": group_w2, "w3_s": w3_s, "w3_v": w3_v,
             "first_0": lambda n: first(n, 0), "first_1": lambda n: first(n, 1),
             "first_2": lambda n: first(n, 2), "first_3": lambda n: first(n, 3),
             "hid_0": lambda n: hidden(n, 0), "hid_1": lambda n: hidden(n, 1),
@@ -449,8 +458,10 @@ def tile_psicritic_pa_kernel(tc, h1_bytes, h1_scale, W2, b2, W3, b3, g1, V2, c2,
         lag_max = max([lag for name, lag in ORDER])
         setup()
         for s in range(lag_min, n_units + lag_max):
-            if s == 0:
+            if s == -SPLIT:
                 setup_biases()
+            if s == 0:
+                bias_columns()
             order = ORDER if s >= 0 else sorted(ORDER, key=lambda e: s - e[1])
             for name, lag in order:
                 n = s - lag
@@ -459,12 +470,12 @@ def tile_psicritic_pa_kernel(tc, h1_bytes, h1_scale, W2, b2, W3, b3, g1, V2, c2,
                 if name == "load_w2" and n == 0:
                     setup_loads()
                     setup_scale()
-                if name == "load_w3" and n == 2 and "R" in KINDS:
+                if name == "load_w3" and n == 2:
                     row_bias_load()
 
         late = [n for n in range(n_units) if kind(n) == "L"]
         turned_items = [(e, i) for k in "AL" for e in range(A // 2) if KINDS[e] == k for i in range(NI)]
-        row_items = [(e, i) for e in range(A // 2) if KINDS[e] == "R" for i in range(NI)]
+        row_items = [(e, i) for e in range(A // 2) if KINDS[e] in "RQ" for i in range(NI)]
         owned = 0
 
         def next_late():
@@ -480,27 +491,46 @@ def tile_psicritic_pa_kernel(tc, h1_bytes, h1_scale, W2, b2, W3, b3, g1, V2, c2,
             nc.vector.scalar_tensor_tensor(
                 out=common[:, h, :], in0=sums[h][:], scalar=-1.0 / A, in1=state_t[:, h, :], op0=MULT, op1=ADD,
             )
+        row_late = [n for n in range(n_units) if kind(n) == "Q"]
+        for n in row_late:
+            own(n, 0)
+            own(n, 1)
         for i in range(0, NI, 2):
             ps = bank("shared_ps")
             view = ps[:].rearrange("p (i h m) -> p i h m", i=2, h=2)
             for j in range(2):
                 for h in range(2):
                     nc.tensor.transpose(view[:, j, h, :], common[:, h, (i + j) * P : (i + j + 1) * P], ident[:])
-            nc.vector.tensor_copy(out=common_rows[:, i : i + 2, :].rearrange("p i s -> p (i s)"), in_=ps[:])
+            shared[i] = ps
+        for n in row_late:
+            own_out(n, 0)
+            if n < row_late[-1] or CROWS == 0:
+                own_out(n, 1)
+        for i in range(0, NI, 2):
+            copy = nc.scalar.copy if i == 2 and CROWS == 1 else nc.vector.tensor_copy
+            copy(out=common_rows[:, i : i + 2, :].rearrange("p i s -> p (i s)"), in_=shared[i][:])
+        if row_late and CROWS != 0:
+            own_out(row_late[-1], 1)
         begun = 0
-        ended = 0
         row = 0
         n_turned, n_row = len(turned_items), len(row_items)
-        while ended < n_turned or row < n_row:
-            while owned < len(late) and 2 * owned < begun + AHEAD * 2:
-                next_late()
-                owned += 1
-            while begun < min(n_turned, ended + 1 + LAG):
-                result_tensor(turned_items[begun])
+        n_early = n_turned - 2 * len(late)
+        while begun < n_turned or row < n_row:
+            run = turned_items[begun : begun + RUN]
+            need = (max(0, begun + len(run) - n_early) + 3) // 4 * 2
+            want = min(len(late), max(need, AHEAD + begun // 2))
+            if owned < need or want >= owned + GROUP or want == len(late):
+                while owned < want:
+                    next_late()
+                    owned += 1
+            for item in run:
+                result_tensor(item)
+            for item in run:
                 begun += 1
-            while row < n_row and (row * n_turned <= ended * n_row or ended == n_turned):
+                while row < n_row and row * n_turned < begun * n_row:
+                    result_out(row_items[row])
+                    row += 1
+                result_out(item)
+            while not run and row < n_row:
                 result_out(row_items[row])
                 row += 1
-            if ended < n_turned:
-                result_out(turned_items[ended])
-                ended += 1

from contextlib import ExitStack

import concourse.mybir as mybir
from concourse.masks import make_identity

B, A, F, S = 512, 16, 512, 256
FLOPS = 2 * B * (A + 1) * (F * F + F * S)

F32 = mybir.dt.float32
BF16 = mybir.dt.bfloat16
U32 = mybir.dt.uint32
U8 = mybir.dt.uint8
FP8 = mybir.dt.float8_e4m3fn
FP8X4 = mybir.dt.float8_e4m3fn_x4
ADD = mybir.AluOpType.add
MAX = mybir.AluOpType.max
MULT = mybir.AluOpType.mult
RELU = mybir.ActivationFunctionType.Relu
IDENT = mybir.ActivationFunctionType.Identity
AXIS_X = mybir.AxisListType.X

P = 128
T = 4
NI = B // P
STATE = A
MANUAL = True
KINDS = "RLLLLLAL"
ORDER = (
    ("quant_x", 0),
    ("quant_w3", 3),
    ("h2_s", 2),
    ("turn_b", -1),
    ("w2", -2),
    ("tc_a", -1),
    ("first_3", 0),
    ("second_out", 5),
    ("widen", -2),
    ("first_2", 0),
    ("load_w3", -2),
    ("first_0", 0),
    ("first_1", 0),
    ("w3_v", 1),
    ("second_b", 4),
    ("quant_w2", -1),
    ("w3_s", -2),
    ("tc_b", -1),
    ("turn_a", -2),
    ("h2_v", 2),
    ("hid_2", 0),
    ("load_x", -3),
    ("hid_0", 0),
    ("load_w2", -4),
    ("quant_h2", 3),
    ("hid_3", 0),
    ("hid_1", 0),
    ("second_a", 4),
)
HA_V = [[0,0,0,0,0],[0]]
HG_S = [[192,256,64,384,352],[192,128,128,256]]
W3_S = [[256],[128,192,64,192]]
SO_V = [[0,0,2,1],[1,1,0,0]]
AHEAD = 3
RUN = 4
GROUP = 2
CROWS = 1
RES = [0,1,2,2]
SPLIT = 2
FAST = True
BUFS = {"x_bytes":2,"w2_raw":2,"w3_raw":4,"x_grp":2,"x_codes":2,"w2_codes":2,"w2_grp":2,"w3_grp":5,"h2_planes":3,"h2_grp":3,"h2_codes":3,"x_scales":2,"w2_scales":2,"x_rows":2,"staged":7}


def tile_psicritic_pa_kernel(tc, h1_bytes, h1_scale, W2, b2, W3, b3, g1, V2, c2, V3, c3, out):
    nc = tc.nc
    units = [STATE] + list(range(A))
    n_units = len(units)
    n_late = 2 * (KINDS.count("L") + KINDS.count("Q"))

    def knob(values, n):
        if n < len(values[0]) - 1:
            return values[0][n]
        back = n_units - 1 - n
        if back < len(values[1]):
            return values[1][back]
        return values[0][-1]

    with ExitStack() as ctx:
        keep = ctx.enter_context(tc.tile_pool(name="keep", bufs=1))
        raw = ctx.enter_context(tc.tile_pool(name="raw", bufs=3))
        work = ctx.enter_context(tc.tile_pool(name="work", bufs=3))
        psum = ctx.enter_context(tc.psum_pool(name="psum", bufs=1))
        if MANUAL:
            ctx.enter_context(tc.manual_schedule())

        def bank(name):
            return psum.tile([P, 512], F32, name=name, tag="ring", bufs=6)

        w3_codes = keep.tile([P, (A + 1) * S], U32, align_bytes=64, name="w3_codes")
        w3_scales = keep.tile([P, (A + 1) * S], U8, align_bytes=64, name="w3_scales")
        ident = keep.tile([P, P], F32, name="ident")
        scale = keep.tile([P, NI, F], F32, align_bytes=64, name="scale")
        b2_rows = keep.tile([P, F], BF16, name="b2_rows")
        b3_rows = keep.tile([P, S], BF16, name="b3_rows")
        b2_f32 = keep.tile([P, F], F32, name="b2_f32")
        b3_f32 = keep.tile([P, S], F32, name="b3_f32")
        b2_col = keep.tile([P, T, A + 1], F32, name="b2_col")
        b3_col = keep.tile([P, 2, A + 1], F32, name="b3_col")
        b3_sum = keep.tile([P, 2], F32, name="b3_sum")
        state_bias = keep.tile([P, 2], F32, name="state_bias")
        state_t = keep.tile([P, 2, B], F32, name="state_t")
        common = keep.tile([P, 2, B], F32, name="common")
        common_rows = keep.tile([P, NI, S], F32, name="common_rows")
        warm = keep.tile([P, 1], F32, name="warm")
        sums = [psum.tile([P, B], F32, name="sum0"), psum.tile([P, B], F32, name="sum1")]

        x_bytes = {}
        x_rows = {}
        w2_raw = {}
        w3_raw = {}
        w2_grp = {}
        w3_grp = {}
        w2_q = {}
        turned = {}
        x_grp = {}
        x_q = {}
        hid = {}
        h2_planes = {}
        h2_grp = {}
        h2_q = {}
        second = {}
        adv = {}
        rows = {}
        b3_wide = {}
        bias_ps = {}
        results = {}
        shared = {}
        staged = {}

        def wt(shape, dtype, name):
            return work.tile(shape, dtype, name=name, align_bytes=64, bufs=BUFS[name])

        def interleave(engine_copy, dst, src):
            if FAST:
                engine_copy(
                    out=dst.rearrange("p (c i) j -> p c j i", i=4),
                    in_=src.rearrange("p j (c i) -> p c j i", i=4),
                )
            else:
                engine_copy(out=dst, in_=src.rearrange("p j c -> p c j"))

        def load_x(n):
            a = units[n]
            if a == STATE:
                t = wt([P, NI, F], BF16, "x_rows")
                nc.sync.dma_start(out=t[:], in_=g1.rearrange("(i p) k -> p i k", p=P))
                x_rows[n] = t
            else:
                t = raw.tile([P, NI, F], U8, name="x_bytes", align_bytes=64, bufs=BUFS["x_bytes"])
                nc.sync.dma_start(out=t[:], in_=h1_bytes[:, a, :].rearrange("(i p) k -> p i k", p=P))
                x_bytes[n] = t

        def load_w2(n):
            a = units[n]
            t = raw.tile([P, T, F], BF16, name="w2_raw", align_bytes=64, bufs=BUFS["w2_raw"])
            nc.sync.dma_start(out=t[:], in_=(V2 if a == STATE else W2[a]).rearrange("(p j) c -> p j c", j=T))
            w2_raw[n] = t

        def load_w3(n):
            a = units[n]
            t = raw.tile([P, T, S], BF16, name="w3_raw", align_bytes=64, bufs=BUFS["w3_raw"])
            nc.sync.dma_start(out=t[:], in_=(V3 if a == STATE else W3[a]).rearrange("(p j) c -> p j c", j=T))
            w3_raw[n] = t

        def widen(n):
            if units[n] == STATE:
                return
            t = wt([P, NI, F], BF16, "x_rows")
            nc.vector.tensor_tensor(
                out=t[:].rearrange("p i k -> p (i k)"),
                in0=x_bytes[n][:].rearrange("p i k -> p (i k)").bitcast(FP8),
                in1=scale[:].rearrange("p i k -> p (i k)"),
                op=MULT,
            )
            x_rows[n] = t

        def turn(n, half):
            ps = bank("turned")
            view = ps[:].rearrange("p (i u r) -> p i u r", i=2, u=2)
            for i in range(2):
                words = x_rows[n][:, 2 * half + i, :].bitcast(F32)
                for u in range(2):
                    nc.tensor.transpose(view[:, i, u, :], words[:, u:256:2], ident[:])
            turned[(n, half)] = view

        def turn_copy(n, half):
            if half == 0:
                x_grp[n] = wt([P, B * T], BF16, "x_grp")
            nc.scalar.copy(
                out=x_grp[n][:, half * 1024 : (half + 1) * 1024].bitcast(F32).rearrange("p (i r u) -> p i r u", i=2, u=2),
                in_=turned[(n, half)].rearrange("p i u r -> p i r u"),
            )

        def quant(codes, scales, grouped):
            nc.vector.quantize_mx(out=codes.bitcast(FP8X4), scales=scales, in_=grouped)

        def quant_x(n):
            codes = wt([P, B], U32, "x_codes")
            scales = wt([P, B], U8, "x_scales")
            quant(codes[:], scales[:], x_grp[n][:])
            x_q[n] = (codes, scales)

        def quant_w2(n):
            codes = wt([P, F], U32, "w2_codes")
            scales = wt([P, F], U8, "w2_scales")
            quant(codes[:], scales[:], w2_grp[n][:])
            w2_q[n] = (codes, scales)

        def quant_w3(n):
            cols = slice(n * S, (n + 1) * S)
            quant(w3_codes[:, cols], w3_scales[:, cols], w3_grp[n][:])

        def group_w3_part(n, engine_copy, lo, hi):
            if lo < hi:
                if n not in w3_grp:
                    w3_grp[n] = wt([P, S * T], BF16, "w3_grp")
                dst = w3_grp[n][:].rearrange("p (c j) -> p c j", j=T)[:, lo:hi, :]
                interleave(engine_copy, dst, w3_raw[n][:, :, lo:hi])

        def w3_s(n):
            group_w3_part(n, nc.scalar.copy, 0, knob(W3_S, n))

        def w3_v(n):
            group_w3_part(n, nc.vector.tensor_copy, knob(W3_S, n), S)

        def group_w2(n):
            w2_grp[n] = wt([P, F * T], BF16, "w2_grp")
            nc.vector.tensor_copy(
                out=w2_grp[n][:].rearrange("p (t v m j) -> p v t j m", t=T, m=2, j=T),
                in_=w2_raw[n][:].rearrange("p j (v m t) -> p v t j m", m=2, t=T),
            )

        def first(n, t):
            x_codes, x_scales = x_q[n]
            codes, scales = w2_q[n]
            ps = bank("hidden")
            nc.tensor.matmul_mx(
                out=ps[:],
                lhsT=codes[:, t * P : (t + 1) * P].bitcast(FP8X4),
                lhsT_scale=scales[:, t * P : (t + 1) * P],
                rhs=x_codes[:].bitcast(FP8X4),
                rhs_scale=x_scales[:],
                start=True,
                stop=True,
            )
            hid[(n, t)] = ps

        def hidden(n, t):
            a = units[n]
            if n not in h2_planes:
                h2_planes[n] = wt([P, T, B], BF16, "h2_planes")
            dst, bias = h2_planes[n][:, t, :], b2_col[:, t, a : a + 1]
            if t >= T - knob(HA_V, n):
                nc.vector.tensor_scalar(out=dst, in0=hid[(n, t)][:], scalar1=bias, scalar2=0.0, op0=ADD, op1=MAX)
            else:
                nc.scalar.activation(out=dst, in_=hid[(n, t)][:], func=RELU, bias=bias, scale=1.0)

        def group_h2_part(n, engine_copy, lo, hi):
            if lo < hi:
                if n not in h2_grp:
                    h2_grp[n] = wt([P, B * T], BF16, "h2_grp")
                dst = h2_grp[n][:].rearrange("p (n j) -> p n j", j=T)[:, lo:hi, :]
                interleave(engine_copy, dst, h2_planes[n][:, :, lo:hi])

        def h2_s(n):
            group_h2_part(n, nc.scalar.copy, 0, knob(HG_S, n))

        def h2_v(n):
            group_h2_part(n, nc.vector.tensor_copy, knob(HG_S, n), B)

        def kind(n):
            return "A" if units[n] == STATE else KINDS[units[n] // 2]

        def quant_h2(n):
            late = kind(n) in "LQ"
            name = "late" if late else "h2"
            codes = work.tile([P, B], U32, name=name + "_codes", align_bytes=64, bufs=n_late if late else BUFS["h2_codes"])
            scales = work.tile([P, B], U8, name=name + "_scales", align_bytes=64, bufs=n_late if late else BUFS["h2_codes"])
            quant(codes[:], scales[:], h2_grp[n][:])
            h2_q[n] = (codes, scales)

        def product2(view, n, h, start, stop):
            codes, scales = h2_q[n]
            cols = slice(n * S + h * P, n * S + (h + 1) * P)
            nc.tensor.matmul_mx(
                out=view,
                lhsT=w3_codes[:, cols].bitcast(FP8X4),
                lhsT_scale=w3_scales[:, cols],
                rhs=codes[:].bitcast(FP8X4),
                rhs_scale=scales[:],
                start=start,
                stop=stop,
            )

        def summed(n, h):
            a = units[n]
            if a != STATE:
                product2(sums[h][:], n, h, a == 0, a == A - 1)

        def own(n, h):
            ps = bank("second")
            second[(n, h)] = ps
            if kind(n) in "RQ":
                codes, scales = h2_q[n]
                cols = slice(n * S, (n + 1) * S)
                for i in range(2):
                    toks = slice((2 * h + i) * P, (2 * h + i + 1) * P)
                    nc.tensor.matmul_mx(
                        out=ps[:, i * S : (i + 1) * S],
                        lhsT=codes[:, toks].bitcast(FP8X4),
                        lhsT_scale=scales[:, toks],
                        rhs=w3_codes[:, cols].bitcast(FP8X4),
                        rhs_scale=w3_scales[:, cols],
                        start=True,
                        stop=True,
                    )
            else:
                product2(ps[:], n, h, True, True)

        def own_out(n, h):
            a = units[n]
            ps = second[(n, h)]
            if kind(n) in "RQ":
                if a % 2 == 0 and h == 0:
                    rows[a // 2] = keep.tile([P, 2, NI, S], F32, name="rows%d" % a)
                nc.vector.tensor_tensor(
                    out=rows[a // 2][:, a % 2, 2 * h : 2 * h + 2, :],
                    in0=ps[:].rearrange("p (i s) -> p i s", i=2),
                    in1=b3_wide[a // 2][:, a % 2 : a % 2 + 1, :].to_broadcast([P, 2, S]),
                    op=ADD,
                )
                return
            if a == STATE:
                dst, bias = state_t[:, h, :], state_bias[:, h : h + 1]
            else:
                if h == 0:
                    if kind(n) == "A":
                        adv[a] = keep.tile([P, 2, B], F32, name="adv%d" % a)
                    else:
                        adv[a] = work.tile([P, 2, B], F32, name="late_adv", bufs=min(n_late, 6))
                dst, bias = adv[a][:, h, :], b3_col[:, h, a : a + 1]
            if kind(n) == "A" and h < knob(SO_V, n):
                nc.vector.tensor_scalar(out=dst, in0=ps[:], scalar1=bias, scalar2=None, op0=ADD)
            else:
                nc.scalar.activation(out=dst, in_=ps[:], func=IDENT, bias=bias, scale=1.0)

        def second_a(n):
            summed(n, 0)
            if kind(n) not in "LQ":
                own(n, 0)

        def second_b(n):
            summed(n, 1)
            if kind(n) not in "LQ":
                own(n, 1)

        def second_out(n):
            if kind(n) not in "LQ":
                own_out(n, 0)
                own_out(n, 1)

        def result_tensor(item):
            e, i = item
            toks = slice(i * P, (i + 1) * P)
            where = RES[len(results) % len(RES)]
            if where == 2:
                ps = bank("result")
            else:
                ps = psum.tile([P, B], F32, name="sum%d" % where)
            view = ps[:].rearrange("p (a h m) -> p a h m", a=2, h=2)
            for j in range(2):
                for h in range(2):
                    nc.tensor.transpose(view[:, j, h, :], adv[2 * e + j][:, h, toks], ident[:])
            results[item] = ps[:].rearrange("p (a s) -> p a s", a=2)

        def result_out(item):
            e, i = item
            dst = work.tile([P, 2, S], F32, name="staged", bufs=BUFS["staged"])
            nc.vector.tensor_tensor(
                out=dst[:],
                in0=rows[e][:, :, i, :] if KINDS[e] in "RQ" else results[item],
                in1=common_rows[:, i : i + 1, :].to_broadcast([P, 2, S]),
                op=ADD,
            )
            nc.sync.dma_start(out=out[i * P : (i + 1) * P, 2 * e : 2 * e + 2, :], in_=dst[:])

        def setup():
            nc.vector.memset(b2_rows[:], 0.0)
            nc.vector.memset(b3_rows[:], 0.0)
            nc.vector.memset(warm[:], 0.0)
            nc.scalar.activation(out=warm[:], in_=warm[:], func=RELU, bias=0.0, scale=1.0)
            make_identity(nc, ident[:])

        def setup_loads():
            nc.sync.dma_start(out=b2_rows[0:A, :], in_=b2)
            nc.sync.dma_start(out=b2_rows[A : A + 1, :], in_=c2.rearrange("(o f) -> o f", o=1))
            nc.sync.dma_start(out=b3_rows[0:A, :], in_=b3)
            nc.sync.dma_start(out=b3_rows[A : A + 1, :], in_=c3.rearrange("(o f) -> o f", o=1))
            nc.sync.dma_start(out=scale[:, 0, :], in_=h1_scale.rearrange("a b k -> (a b k)").partition_broadcast(P))

        def row_bias_load():
            for e in range(A // 2):
                if KINDS[e] in "RQ":
                    b3_wide[e] = keep.tile([P, 2, S], BF16, name="b3_wide%d" % e)
                    nc.sync.dma_start(
                        out=b3_wide[e][:].rearrange("p a s -> p (a s)"),
                        in_=b3[2 * e : 2 * e + 2, :].rearrange("a s -> (a s)").partition_broadcast(P),
                    )

        def setup_scale():
            for i in range(1, NI):
                nc.scalar.copy(out=scale[:, i, :], in_=scale[:, 0, :])

        def setup_biases():
            nc.vector.tensor_copy(out=b2_f32[:], in_=b2_rows[:])
            nc.vector.tensor_copy(out=b3_f32[:], in_=b3_rows[:])
            ps = bank("bias2")
            view = ps[:].rearrange("p (t a) -> p t a", t=T)
            for t in range(T):
                nc.tensor.transpose(view[:, t, :], b2_f32[:, t:F:T], ident[:])
            ps3 = bank("bias3")
            view3 = ps3[:, 0:256].rearrange("p (h a) -> p h a", h=2)
            for h in range(2):
                nc.tensor.transpose(view3[:, h, :], b3_f32[:, h * P : (h + 1) * P], ident[:])
            bias_ps[0] = (view, view3)

        def bias_columns():
            view, view3 = bias_ps[0]
            nc.vector.tensor_copy(out=b2_col[:], in_=view[:, :, 0 : A + 1])
            nc.vector.tensor_copy(out=b3_col[:], in_=view3[:, :, 0 : A + 1])
            nc.vector.reduce_sum(out=b3_sum[:], in_=b3_col[:, :, 0:A], axis=AXIS_X)
            nc.vector.scalar_tensor_tensor(
                out=state_bias[:], in0=b3_sum[:], scalar=-1.0 / A, in1=b3_col[:, :, A], op0=MULT, op1=ADD,
            )

        stages = {
            "load_x": load_x, "load_w2": load_w2, "load_w3": load_w3, "widen": widen,
            "turn_a": lambda n: turn(n, 0), "turn_b": lambda n: turn(n, 1),
            "tc_a": lambda n: turn_copy(n, 0), "tc_b": lambda n: turn_copy(n, 1),
            "quant_x": quant_x, "quant_w2": quant_w2, "quant_w3": quant_w3,
            "w2": group_w2, "w3_s": w3_s, "w3_v": w3_v,
            "first_0": lambda n: first(n, 0), "first_1": lambda n: first(n, 1),
            "first_2": lambda n: first(n, 2), "first_3": lambda n: first(n, 3),
            "hid_0": lambda n: hidden(n, 0), "hid_1": lambda n: hidden(n, 1),
            "hid_2": lambda n: hidden(n, 2), "hid_3": lambda n: hidden(n, 3),
            "h2_s": h2_s, "h2_v": h2_v, "quant_h2": quant_h2,
            "second_a": second_a, "second_b": second_b, "second_out": second_out,
        }
        lag_min = min([lag for name, lag in ORDER])
        lag_max = max([lag for name, lag in ORDER])
        setup()
        for s in range(lag_min, n_units + lag_max):
            if s == -SPLIT:
                setup_biases()
            if s == 0:
                bias_columns()
            order = ORDER if s >= 0 else sorted(ORDER, key=lambda e: s - e[1])
            for name, lag in order:
                n = s - lag
                if 0 <= n < n_units:
                    stages[name](n)
                if name == "load_w2" and n == 0:
                    setup_loads()
                    setup_scale()
                if name == "load_w3" and n == 2:
                    row_bias_load()

        late = [n for n in range(n_units) if kind(n) == "L"]
        turned_items = [(e, i) for k in "AL" for e in range(A // 2) if KINDS[e] == k for i in range(NI)]
        row_items = [(e, i) for e in range(A // 2) if KINDS[e] in "RQ" for i in range(NI)]
        owned = 0

        def next_late():
            own(late[owned], 0)
            own(late[owned], 1)
            own_out(late[owned], 0)
            own_out(late[owned], 1)

        while owned < min(AHEAD, len(late)):
            next_late()
            owned += 1
        for h in range(2):
            nc.vector.scalar_tensor_tensor(
                out=common[:, h, :], in0=sums[h][:], scalar=-1.0 / A, in1=state_t[:, h, :], op0=MULT, op1=ADD,
            )
        row_late = [n for n in range(n_units) if kind(n) == "Q"]
        for n in row_late:
            own(n, 0)
            own(n, 1)
        for i in range(0, NI, 2):
            ps = bank("shared_ps")
            view = ps[:].rearrange("p (i h m) -> p i h m", i=2, h=2)
            for j in range(2):
                for h in range(2):
                    nc.tensor.transpose(view[:, j, h, :], common[:, h, (i + j) * P : (i + j + 1) * P], ident[:])
            shared[i] = ps
        for n in row_late:
            own_out(n, 0)
            if n < row_late[-1] or CROWS == 0:
                own_out(n, 1)
        for i in range(0, NI, 2):
            copy = nc.scalar.copy if i == 2 and CROWS == 1 else nc.vector.tensor_copy
            copy(out=common_rows[:, i : i + 2, :].rearrange("p i s -> p (i s)"), in_=shared[i][:])
        if row_late and CROWS != 0:
            own_out(row_late[-1], 1)
        begun = 0
        row = 0
        n_turned, n_row = len(turned_items), len(row_items)
        n_early = n_turned - 2 * len(late)
        while begun < n_turned or row < n_row:
            run = turned_items[begun : begun + RUN]
            need = (max(0, begun + len(run) - n_early) + 3) // 4 * 2
            want = min(len(late), max(need, AHEAD + begun // 2))
            if owned < need or want >= owned + GROUP or want == len(late):
                while owned < want:
                    next_late()
                    owned += 1
            for item in run:
                result_tensor(item)
            for item in run:
                begun += 1
                while row < n_row and row * n_turned < begun * n_row:
                    result_out(row_items[row])
                    row += 1
                result_out(item)
            while not run and row < n_row:
                result_out(row_items[row])
                row += 1
